import numpy as np
import ml_dtypes


def mxq(x, axis, fmt="e4m3"):
    dtype, down = {"e4m3": (ml_dtypes.float8_e4m3fn, 7), "e5m2": (ml_dtypes.float8_e5m2, 14)}[fmt]
    v = np.moveaxis(np.asarray(x, np.float32).astype(ml_dtypes.bfloat16).astype(np.float64), axis, -1)
    blocks = v.reshape(v.shape[:-1] + (-1, 32))
    amax = np.abs(blocks).max(-1, keepdims=True)
    byte = np.maximum(np.where(amax > 0, np.frexp(amax)[1] - 1 + 127, 0) - down, 1)
    scale = np.exp2(byte - 127.0)
    codes = (blocks / scale).astype(np.float32).astype(dtype).astype(np.float64)
    return np.moveaxis((codes * scale).reshape(v.shape), -1, axis)


WIDE = False


def mx_kscale(k):
    if not WIDE:
        return np.ones(k)
    levels = np.array([10, -10, 5, -5, 0])
    a = np.random.permutation(np.resize(levels, k // 512 * 4)).reshape(k // 512, 4)
    idx = np.arange(k)
    return np.exp2(a[idx // 512, idx % 128 // 32])


BF16 = ml_dtypes.bfloat16


def bf(x):
    return np.asarray(x, np.float32).astype(BF16)


def f64(x):
    return np.asarray(x).astype(np.float64)


B, H, W, C, F, KH, KW, G, P = 32, 18, 18, 64, 128, 3, 3, 5, 3
HO, WO = H - KH + 1, W - KW + 1
NB = G + P
IN = KH * KW * C
GRID_MIN, GRID_MAX = -1.0, 1.0


def knots():
    h = (GRID_MAX - GRID_MIN) / G
    return np.linspace(GRID_MIN - P * h, GRID_MAX + P * h, G + 2 * P + 1)


def spline_basis(v):
    t = knots()
    v = v[..., None]
    b = np.where((v >= t[:-1]) & (v < t[1:]), 1.0, 0.0)
    for k in range(1, P + 1):
        b = ((v - t[:-(k + 1)]) / (t[k:-1] - t[:-(k + 1)]) * b[..., :-1]
             + (t[k + 1:] - v) / (t[k + 1:] - t[1:-k]) * b[..., 1:])
    return b


def setup_inputs():
    t = knots()
    a = np.maximum(np.log2(mx_kscale(C * NB)[::NB]), 0.0)
    x0 = np.random.standard_normal((B, H, W, C))
    sgn = np.where(np.random.standard_normal((B, H, W, C)) < 0.0, -1.0, 1.0)
    edge = sgn * (t[-1] - (t[1] - t[0]) * 2.0 ** (-a / 2.0))
    x = bf(np.where(a > 0.0, edge, x0))
    peak = spline_basis(f64(x)).max(axis=-1).reshape(B * H * W, C).max(axis=0)
    r = np.where(a > 0.0, 2.0 ** np.round(-np.log2(peak)), 1.0)
    rows = np.tile(r, KH * KW)
    return {"x": x,
            "spline_kernel": bf(np.random.standard_normal((IN, NB, F)) * rows[:, None, None]),
            "scale_factor": bf(np.random.standard_normal((IN, F)) / np.sqrt(IN)),
            "base": bf(np.random.standard_normal((B, HO, WO, F)) * 0.6),
            "kan_bias": bf(np.random.standard_normal(F) * 0.2),
            "conv_bias": bf(np.random.standard_normal(F) * 0.2)}


def reference(x, spline_kernel, scale_factor, base, kan_bias, conv_bias):
    sb = spline_basis(f64(x))
    sq = mxq(sb.reshape(B * H * W, C * NB), 1, "e4m3").reshape(B, H, W, C * NB)
    w = f64(spline_kernel) * f64(scale_factor)[:, None, :]
    wq = mxq(w.reshape(KH * KW, C * NB, F), 1, "e4m3")
    spl = 0.0
    for di in range(KH):
        for dj in range(KW):
            win = sq[:, di:di + HO, dj:dj + WO, :].reshape(B * HO * WO, C * NB)
            spl = spl + (win @ wq[di * KW + dj])
    out = spl.reshape(B, HO, WO, F) + f64(base) + f64(kan_bias)
    return out + f64(conv_bias)

@@ -1,0 +1,280 @@
+from contextlib import ExitStack
+
+import concourse.mybir as mybir
+from concourse.masks import make_identity
+
+F32 = mybir.dt.float32
+BF16 = mybir.dt.bfloat16
+I32 = mybir.dt.int32
+U32 = mybir.dt.uint32
+U8 = mybir.dt.uint8
+FP8X4 = mybir.dt.float8_e4m3fn_x4
+ALU = mybir.AluOpType
+ACT = mybir.ActivationFunctionType
+
+P = 128
+IMAGES, SIDE, C, F = 32, 18, 64, 128
+OUT_SIDE = SIDE - 2
+TAPS = 9
+SPOTS = SIDE * SIDE
+COLS = SPOTS * IMAGES
+ROW_COLS = SIDE * IMAGES
+SPOTS_PER_TILE = P // IMAGES
+BLOCKS = COLS // P
+CHUNK = 512
+Q_TILES = OUT_SIDE // SPOTS_PER_TILE
+X_LOADS = 4
+
+FLOPS = 2 * IMAGES * OUT_SIDE * OUT_SIDE * TAPS * C * 8 * F
+
+
+def tile_conv2dkan_pa_t_kernel(
+    tc, x, spline_kernel, scale_factor, base, kan_bias, conv_bias, out
+):
+    nc = tc.nc
+    with ExitStack() as stack:
+        keep = stack.enter_context(tc.tile_pool(name="keep", bufs=1))
+        work = stack.enter_context(tc.tile_pool(name="work", bufs=2))
+        psum_x = stack.enter_context(tc.psum_pool(name="psum_x", bufs=2))
+        psum_z = stack.enter_context(tc.psum_pool(name="psum_z", bufs=4))
+        psum_out = stack.enter_context(tc.psum_pool(name="psum_out", bufs=2))
+
+        x_blocks = keep.tile([P, BLOCKS, P], BF16)
+        nc.vector.memset(x_blocks[:, :, C:P], 0.0)
+        nc.vector.memset(x_blocks[:, :, C : C + 1], 1.0)
+        x_by_spot = x.rearrange("b h w c -> b (h w) c").rearrange(
+            "b (n s) c -> s b n c", s=SPOTS_PER_TILE
+        )
+        blocks_per_load = -(-BLOCKS // X_LOADS)
+        for first in range(0, BLOCKS, blocks_per_load):
+            last = min(first + blocks_per_load, BLOCKS)
+            for s in range(SPOTS_PER_TILE):
+                nc.sync.dma_start(
+                    out=x_blocks[s * IMAGES : (s + 1) * IMAGES, first:last, 0:C],
+                    in_=x_by_spot[s, :, first:last, :],
+                )
+
+        identity = keep.tile([P, P], BF16)
+        make_identity(nc, identity[:])
+        to_z = keep.tile([P, 2, C, 2], BF16)
+        for lo in range(2):
+            nc.vector.tensor_scalar(
+                out=to_z[:, lo],
+                in0=identity[:, 0:C].unsqueeze(2).to_broadcast([P, C, 2]),
+                scalar1=2.5,
+                scalar2=None,
+                op0=ALU.mult,
+            )
+            for hi in range(2):
+                nc.vector.memset(to_z[C : C + 1, lo, :, hi], 1.5 - 2 * hi - lo)
+
+        kernel_raw = keep.tile([P, 2, TAPS, 2, F], BF16)
+        factor_raw = keep.tile([P, TAPS, F], BF16)
+        kernel_view = spline_kernel.rearrange(
+            "(tap c) (half hi lo) o -> hi half c tap lo o", c=C, half=2, hi=2
+        )
+        factor_view = scale_factor.rearrange("(tap c) o -> c tap o", c=C)
+        for hi in range(2):
+            nc.sync.dma_start(out=factor_raw[hi:P:2], in_=factor_view)
+            for half in range(2):
+                nc.sync.dma_start(out=kernel_raw[hi:P:2, half], in_=kernel_view[hi, half])
+        w_grouped = keep.tile([P, TAPS, F, 2, 2], BF16, align_bytes=64)
+        w_codes = keep.tile([P, TAPS, F], U32, align_bytes=64)
+        w_scales = keep.tile([P, TAPS, F], U8, align_bytes=64)
+        for tap in range(TAPS):
+            nc.vector.tensor_tensor(
+                out=w_grouped[:, tap],
+                in0=kernel_raw[:, :, tap].rearrange("p half lo o -> p o half lo"),
+                in1=factor_raw[:, tap].unsqueeze(2).unsqueeze(3).to_broadcast([P, F, 2, 2]),
+                op=ALU.mult,
+            )
+        for tap in range(TAPS):
+            nc.vector.quantize_mx(
+                out=w_codes[:, tap].bitcast(FP8X4),
+                scales=w_scales[:, tap],
+                in_=w_grouped[:, tap].rearrange("p o half lo -> p (o half lo)"),
+            )
+
+        base_tiles = keep.tile([P, OUT_SIDE * Q_TILES, F], BF16)
+        base_view = base.rearrange("b p (t j) o -> j b (p t) o", j=SPOTS_PER_TILE)
+        out_view = out.rearrange("b p (t j) o -> j b p t o", j=SPOTS_PER_TILE)
+        kan_rows = keep.tile([P, F], BF16)
+        conv_rows = keep.tile([P, F], BF16)
+        nc.sync.dma_start(out=kan_rows[:], in_=kan_bias.partition_broadcast(P))
+        nc.sync.dma_start(out=conv_rows[:], in_=conv_bias.partition_broadcast(P))
+        bias_rows = keep.tile([P, F], F32)
+        nc.gpsimd.tensor_tensor(out=bias_rows[:], in0=kan_rows[:], in1=conv_rows[:], op=ALU.add)
+        for j in range(SPOTS_PER_TILE):
+            nc.sync.dma_start(
+                out=base_tiles[j * IMAGES : (j + 1) * IMAGES], in_=base_view[j]
+            )
+
+        sb_codes = keep.tile([P, COLS], U32, align_bytes=64)
+        sb_scales = keep.tile([P, COLS], U8, align_bytes=64)
+        sb_scales_moved = keep.tile([P, COLS + 64], U8, align_bytes=64)
+        nc.vector.memset(sb_scales[:].bitcast(I32), 0)
+
+        def knot_offsets(start, width):
+            x_t_psum = psum_x.tile([P, CHUNK], BF16)
+            for i in range(width // P):
+                nc.tensor.transpose(
+                    x_t_psum[:, i * P : (i + 1) * P], x_blocks[:, start // P + i, :], identity[:]
+                )
+            x_t = work.tile([P, CHUNK], BF16)
+            nc.scalar.copy(out=x_t[:, :width], in_=x_t_psum[:, :width])
+            z_tiles = []
+            for lo in range(2):
+                z = psum_z.tile([P, CHUNK], F32, name="z")
+                nc.tensor.matmul(
+                    z[:, :width],
+                    lhsT=to_z[:, lo].rearrange("r c hi -> r (c hi)"),
+                    rhs=x_t[:, :width],
+                    start=True,
+                    stop=True,
+                )
+                z_tiles.append(z)
+            return z_tiles
+
+        def quantised_basis(start, width, z_tiles):
+            from_knot = work.tile([P, 2, CHUNK], F32)
+            side = work.tile([P, 2, CHUNK], BF16)
+            for lo in range(2):
+                nc.scalar.activation(
+                    out=from_knot[:, lo, :width], in_=z_tiles[lo][:, :width], func=ACT.Abs
+                )
+                nc.scalar.activation(
+                    out=side[:, lo, :width], in_=z_tiles[lo][:, :width], func=ACT.Sign
+                )
+            from_peak = work.tile([P, 2, CHUNK], F32)
+            nc.scalar.activation(
+                out=from_peak[:, :, :width], in_=from_knot[:, :, :width], func=ACT.Abs, bias=-2.0
+            )
+            peak_sq = work.tile([P, 2, CHUNK], F32)
+            nc.scalar.activation(
+                out=peak_sq[:, :, :width], in_=from_knot[:, :, :width], func=ACT.Square, bias=-2.0
+            )
+            hat_sq = work.tile([P, 2, CHUNK], F32)
+            nc.scalar.activation(
+                out=hat_sq[:, :, :width], in_=from_peak[:, :, :width], func=ACT.Square, bias=-2.0
+            )
+            neg_hat = work.tile([P, 2, CHUNK], F32)
+            nc.vector.tensor_scalar(
+                out=neg_hat[:, :, :width],
+                in0=from_peak[:, :, :width],
+                scalar1=2.0,
+                scalar2=0.0,
+                op0=ALU.subtract,
+                op1=ALU.min,
+            )
+            outer = work.tile([P, 2, CHUNK], F32)
+            nc.vector.scalar_tensor_tensor(
+                out=outer[:, :, :width],
+                in0=neg_hat[:, :, :width],
+                scalar=-1.0 / 6.0,
+                in1=hat_sq[:, :, :width],
+                op0=ALU.mult,
+                op1=ALU.mult,
+            )
+            inner = work.tile([P, 2, CHUNK], F32)
+            nc.vector.scalar_tensor_tensor(
+                out=inner[:, :, :width],
+                in0=neg_hat[:, :, :width],
+                scalar=0.5,
+                in1=peak_sq[:, :, :width],
+                op0=ALU.mult,
+                op1=ALU.mult,
+            )
+            bump = work.tile([P, 2, CHUNK], BF16)
+            nc.vector.scalar_tensor_tensor(
+                out=bump[:, :, :width],
+                in0=inner[:, :, :width],
+                scalar=2.0 / 3.0,
+                in1=outer[:, :, :width],
+                op0=ALU.add,
+                op1=ALU.min,
+            )
+            chosen = work.tile([P, 2, 2, CHUNK], BF16)
+            nc.vector.tensor_scalar(
+                out=chosen[:, 0, :, :width],
+                in0=side[:, :, :width],
+                scalar1=-1.0,
+                scalar2=0.0,
+                op0=ALU.mult,
+                op1=ALU.max,
+            )
+            nc.vector.tensor_scalar(
+                out=chosen[:, 1, :, :width],
+                in0=side[:, :, :width],
+                scalar1=0.0,
+                scalar2=None,
+                op0=ALU.max,
+            )
+            grouped = work.tile([P, CHUNK, 2, 2], BF16, align_bytes=64)
+            nc.vector.tensor_tensor(
+                out=grouped[:, :width],
+                in0=bump[:, :, :width]
+                .rearrange("p lo n -> p n lo")
+                .unsqueeze(2)
+                .to_broadcast([P, width, 2, 2]),
+                in1=chosen[:, :, :, :width].rearrange("p half lo n -> p n half lo"),
+                op=ALU.mult,
+            )
+            columns = slice(start, start + width)
+            nc.vector.quantize_mx(
+                out=sb_codes[:, columns].bitcast(FP8X4),
+                scales=sb_scales[:, columns],
+                in_=grouped[:, :width].rearrange("p n half lo -> p (n half lo)"),
+            )
+            nc.vector.tensor_copy(
+                out=sb_scales_moved[:, start + IMAGES : start + IMAGES + width].bitcast(I32),
+                in_=sb_scales[:, columns].bitcast(I32),
+            )
+
+        def output_row(p):
+            acc = psum_out.tile([P, Q_TILES, F], F32)
+            for t in range(Q_TILES):
+                for tap in range(TAPS):
+                    di, dj = divmod(tap, 3)
+                    first = ((p + di) * SIDE + t * SPOTS_PER_TILE + dj) * IMAGES
+                    if first % 64 == 0:
+                        window_scales = sb_scales[:, first : first + P]
+                    else:
+                        window_scales = sb_scales_moved[:, first + IMAGES : first + IMAGES + P]
+                    nc.tensor.matmul_mx(
+                        out=acc[:, t, :],
+                        lhsT=sb_codes[:, first : first + P].bitcast(FP8X4),
+                        lhsT_scale=window_scales,
+                        rhs=w_codes[:, tap].bitcast(FP8X4),
+                        rhs_scale=w_scales[:, tap],
+                        start=(tap == 0),
+                        stop=(tap == TAPS - 1),
+                    )
+            added = work.tile([P, Q_TILES, F], F32)
+            nc.gpsimd.tensor_tensor(
+                out=added[:],
+                in0=base_tiles[:, p * Q_TILES : (p + 1) * Q_TILES, :],
+                in1=bias_rows[:].unsqueeze(1).to_broadcast([P, Q_TILES, F]),
+                op=ALU.add,
+            )
+            result = work.tile([P, Q_TILES, F], F32)
+            nc.vector.tensor_tensor(out=result[:], in0=acc[:], in1=added[:], op=ALU.add)
+            for j in range(SPOTS_PER_TILE):
+                nc.sync.dma_start(
+                    out=out_view[j, :, p], in_=result[j * IMAGES : (j + 1) * IMAGES]
+                )
+
+        starts = list(range(0, COLS, CHUNK))
+        widths = [min(CHUNK, COLS - start) for start in starts]
+        next_row = 0
+        z_next = knot_offsets(starts[0], widths[0])
+        for i, start in enumerate(starts):
+            z_now = z_next
+            if i + 1 < len(starts):
+                z_next = knot_offsets(starts[i + 1], widths[i + 1])
+            while (next_row + 3) * ROW_COLS <= start:
+                output_row(next_row)
+                next_row += 1
+            quantised_basis(start, widths[i], z_now)
+        while next_row < OUT_SIDE:
+            output_row(next_row)
+            next_row += 1

@@ -23,6 +23,7 @@ SPOTS_PER_TILE = P // IMAGES
 BLOCKS = COLS // P
 CHUNK = 512
 Q_TILES = OUT_SIDE // SPOTS_PER_TILE
+RUN = 4
 X_LOADS = 4
 
 FLOPS = 2 * IMAGES * OUT_SIDE * OUT_SIDE * TAPS * C * 8 * F
@@ -193,37 +194,33 @@ def tile_conv2dkan_pa_t_kernel(
                 op0=ALU.add,
                 op1=ALU.min,
             )
-            chosen = work.tile([P, 2, 2, CHUNK], BF16)
-            nc.vector.tensor_scalar(
-                out=chosen[:, 0, :, :width],
-                in0=side[:, :, :width],
-                scalar1=-1.0,
-                scalar2=0.0,
-                op0=ALU.mult,
-                op1=ALU.max,
+            signed = work.tile([P, 4, CHUNK], BF16)
+            nc.vector.tensor_tensor(
+                out=signed[:, 2:4, :width],
+                in0=bump[:, :, :width],
+                in1=side[:, :, :width],
+                op=ALU.mult,
             )
             nc.vector.tensor_scalar(
-                out=chosen[:, 1, :, :width],
-                in0=side[:, :, :width],
+                out=signed[:, 0:2, :width],
+                in0=signed[:, 2:4, :width],
+                scalar1=-1.0,
+                scalar2=None,
+                op0=ALU.mult,
+            )
+            grouped = work.tile([P, CHUNK, 4], BF16, align_bytes=64)
+            nc.vector.tensor_scalar(
+                out=grouped[:, :width].rearrange("p (c i) t -> p c t i", i=RUN),
+                in0=signed[:, :, :width].rearrange("p t (c i) -> p c t i", i=RUN),
                 scalar1=0.0,
                 scalar2=None,
                 op0=ALU.max,
-            )
-            grouped = work.tile([P, CHUNK, 2, 2], BF16, align_bytes=64)
-            nc.vector.tensor_tensor(
-                out=grouped[:, :width],
-                in0=bump[:, :, :width]
-                .rearrange("p lo n -> p n lo")
-                .unsqueeze(2)
-                .to_broadcast([P, width, 2, 2]),
-                in1=chosen[:, :, :, :width].rearrange("p half lo n -> p n half lo"),
-                op=ALU.mult,
             )
             columns = slice(start, start + width)
             nc.vector.quantize_mx(
                 out=sb_codes[:, columns].bitcast(FP8X4),
                 scales=sb_scales[:, columns],
-                in_=grouped[:, :width].rearrange("p n half lo -> p (n half lo)"),
+                in_=grouped[:, :width].rearrange("p n t -> p (n t)"),
             )
             nc.vector.tensor_copy(
                 out=sb_scales_moved[:, start + IMAGES : start + IMAGES + width].bitcast(I32),

@@ -34,6 +34,7 @@ def tile_conv2dkan_pa_t_kernel(
 ):
     nc = tc.nc
     with ExitStack() as stack:
+        stack.enter_context(tc.manual_schedule())
         keep = stack.enter_context(tc.tile_pool(name="keep", bufs=1))
         work = stack.enter_context(tc.tile_pool(name="work", bufs=2))
         psum_x = stack.enter_context(tc.psum_pool(name="psum_x", bufs=2))
@@ -41,13 +42,13 @@ def tile_conv2dkan_pa_t_kernel(
         psum_out = stack.enter_context(tc.psum_pool(name="psum_out", bufs=2))
 
         x_blocks = keep.tile([P, BLOCKS, P], BF16)
-        nc.vector.memset(x_blocks[:, :, C:P], 0.0)
-        nc.vector.memset(x_blocks[:, :, C : C + 1], 1.0)
         x_by_spot = x.rearrange("b h w c -> b (h w) c").rearrange(
             "b (n s) c -> s b n c", s=SPOTS_PER_TILE
         )
         blocks_per_load = -(-BLOCKS // X_LOADS)
-        for first in range(0, BLOCKS, blocks_per_load):
+
+        def load_x(piece):
+            first = piece * blocks_per_load
             last = min(first + blocks_per_load, BLOCKS)
             for s in range(SPOTS_PER_TILE):
                 nc.sync.dma_start(
@@ -55,6 +56,32 @@ def tile_conv2dkan_pa_t_kernel(
                     in_=x_by_spot[s, :, first:last, :],
                 )
 
+        kernel_raw = keep.tile([P, 2, TAPS, 2, F], BF16)
+        factor_raw = keep.tile([P, TAPS, F], BF16)
+        kernel_view = spline_kernel.rearrange(
+            "(tap c) (half hi lo) o -> hi half c tap lo o", c=C, half=2, hi=2
+        )
+        factor_view = scale_factor.rearrange("(tap c) o -> c tap o", c=C)
+        base_tiles = keep.tile([P, OUT_SIDE * Q_TILES, F], BF16)
+        base_view = base.rearrange("b p (t j) o -> j b (p t) o", j=SPOTS_PER_TILE)
+        out_view = out.rearrange("b p (t j) o -> j b p t o", j=SPOTS_PER_TILE)
+        kan_rows = keep.tile([P, F], BF16)
+        conv_rows = keep.tile([P, F], BF16)
+
+        load_x(0)
+        for hi in range(2):
+            nc.sync.dma_start(out=factor_raw[hi:P:2], in_=factor_view)
+            for half in range(2):
+                nc.sync.dma_start(out=kernel_raw[hi:P:2, half], in_=kernel_view[hi, half])
+        for piece in range(1, X_LOADS):
+            load_x(piece)
+        nc.sync.dma_start(out=kan_rows[:], in_=kan_bias.partition_broadcast(P))
+        nc.sync.dma_start(out=conv_rows[:], in_=conv_bias.partition_broadcast(P))
+        for j in range(SPOTS_PER_TILE):
+            nc.sync.dma_start(out=base_tiles[j * IMAGES : (j + 1) * IMAGES], in_=base_view[j])
+
+        nc.vector.memset(x_blocks[:, :, C:P], 0.0)
+        nc.vector.memset(x_blocks[:, :, C : C + 1], 1.0)
         identity = keep.tile([P, P], BF16)
         make_identity(nc, identity[:])
         to_z = keep.tile([P, 2, C, 2], BF16)
@@ -66,19 +93,15 @@ def tile_conv2dkan_pa_t_kernel(
                 scalar2=None,
                 op0=ALU.mult,
             )
+        for lo in range(2):
             for hi in range(2):
                 nc.vector.memset(to_z[C : C + 1, lo, :, hi], 1.5 - 2 * hi - lo)
 
-        kernel_raw = keep.tile([P, 2, TAPS, 2, F], BF16)
-        factor_raw = keep.tile([P, TAPS, F], BF16)
-        kernel_view = spline_kernel.rearrange(
-            "(tap c) (half hi lo) o -> hi half c tap lo o", c=C, half=2, hi=2
-        )
-        factor_view = scale_factor.rearrange("(tap c) o -> c tap o", c=C)
-        for hi in range(2):
-            nc.sync.dma_start(out=factor_raw[hi:P:2], in_=factor_view)
-            for half in range(2):
-                nc.sync.dma_start(out=kernel_raw[hi:P:2, half], in_=kernel_view[hi, half])
+        sb_codes = keep.tile([P, COLS], U32, align_bytes=64)
+        sb_scales = keep.tile([P, COLS], U8, align_bytes=64)
+        sb_scales_moved = keep.tile([P, COLS + 64], U8, align_bytes=64)
+        nc.vector.memset(sb_scales[:].bitcast(I32), 0)
+
         w_grouped = keep.tile([P, TAPS, F, 2, 2], BF16, align_bytes=64)
         w_codes = keep.tile([P, TAPS, F], U32, align_bytes=64)
         w_scales = keep.tile([P, TAPS, F], U8, align_bytes=64)
@@ -95,56 +118,53 @@ def tile_conv2dkan_pa_t_kernel(
                 scales=w_scales[:, tap],
                 in_=w_grouped[:, tap].rearrange("p o half lo -> p (o half lo)"),
             )
-
-        base_tiles = keep.tile([P, OUT_SIDE * Q_TILES, F], BF16)
-        base_view = base.rearrange("b p (t j) o -> j b (p t) o", j=SPOTS_PER_TILE)
-        out_view = out.rearrange("b p (t j) o -> j b p t o", j=SPOTS_PER_TILE)
-        kan_rows = keep.tile([P, F], BF16)
-        conv_rows = keep.tile([P, F], BF16)
-        nc.sync.dma_start(out=kan_rows[:], in_=kan_bias.partition_broadcast(P))
-        nc.sync.dma_start(out=conv_rows[:], in_=conv_bias.partition_broadcast(P))
         bias_rows = keep.tile([P, F], F32)
-        nc.gpsimd.tensor_tensor(out=bias_rows[:], in0=kan_rows[:], in1=conv_rows[:], op=ALU.add)
-        for j in range(SPOTS_PER_TILE):
-            nc.sync.dma_start(
-                out=base_tiles[j * IMAGES : (j + 1) * IMAGES], in_=base_view[j]
-            )
 
-        sb_codes = keep.tile([P, COLS], U32, align_bytes=64)
-        sb_scales = keep.tile([P, COLS], U8, align_bytes=64)
-        sb_scales_moved = keep.tile([P, COLS + 64], U8, align_bytes=64)
-        nc.vector.memset(sb_scales[:].bitcast(I32), 0)
+        starts = list(range(0, COLS, CHUNK))
+        widths = [min(CHUNK, COLS - start) for start in starts]
+        chunks = len(starts)
+        x_t_psum_of = {}
+        x_t_of = {}
+        z_of = {}
+        scalar_out_of = {}
 
-        def knot_offsets(start, width):
+        def transpose_x(i):
             x_t_psum = psum_x.tile([P, CHUNK], BF16)
-            for i in range(width // P):
+            for n in range(widths[i] // P):
                 nc.tensor.transpose(
-                    x_t_psum[:, i * P : (i + 1) * P], x_blocks[:, start // P + i, :], identity[:]
+                    x_t_psum[:, n * P : (n + 1) * P], x_blocks[:, starts[i] // P + n, :], identity[:]
                 )
+            x_t_psum_of[i] = x_t_psum
+
+        def copy_x_t(i):
             x_t = work.tile([P, CHUNK], BF16)
-            nc.scalar.copy(out=x_t[:, :width], in_=x_t_psum[:, :width])
-            z_tiles = []
+            nc.scalar.copy(out=x_t[:, : widths[i]], in_=x_t_psum_of[i][:, : widths[i]])
+            x_t_of[i] = x_t
+
+        def knot_offsets(i):
+            z_of[i] = []
             for lo in range(2):
                 z = psum_z.tile([P, CHUNK], F32, name="z")
                 nc.tensor.matmul(
-                    z[:, :width],
+                    z[:, : widths[i]],
                     lhsT=to_z[:, lo].rearrange("r c hi -> r (c hi)"),
-                    rhs=x_t[:, :width],
+                    rhs=x_t_of[i][:, : widths[i]],
                     start=True,
                     stop=True,
                 )
-                z_tiles.append(z)
-            return z_tiles
+                z_of[i].append(z)
 
-        def quantised_basis(start, width, z_tiles):
+        def scalar_part(i):
+            width = widths[i]
             from_knot = work.tile([P, 2, CHUNK], F32)
             side = work.tile([P, 2, CHUNK], BF16)
             for lo in range(2):
                 nc.scalar.activation(
-                    out=from_knot[:, lo, :width], in_=z_tiles[lo][:, :width], func=ACT.Abs
+                    out=from_knot[:, lo, :width], in_=z_of[i][lo][:, :width], func=ACT.Abs
                 )
+            for lo in range(2):
                 nc.scalar.activation(
-                    out=side[:, lo, :width], in_=z_tiles[lo][:, :width], func=ACT.Sign
+                    out=side[:, lo, :width], in_=z_of[i][lo][:, :width], func=ACT.Sign
                 )
             from_peak = work.tile([P, 2, CHUNK], F32)
             nc.scalar.activation(
@@ -154,80 +174,92 @@ def tile_conv2dkan_pa_t_kernel(
             nc.scalar.activation(
                 out=peak_sq[:, :, :width], in_=from_knot[:, :, :width], func=ACT.Square, bias=-2.0
             )
+            hat = work.tile([P, 2, CHUNK], F32)
+            nc.scalar.activation(
+                out=hat[:, :, :width],
+                in_=from_peak[:, :, :width],
+                func=ACT.Relu,
+                bias=2.0,
+                scale=-1.0,
+            )
             hat_sq = work.tile([P, 2, CHUNK], F32)
             nc.scalar.activation(
                 out=hat_sq[:, :, :width], in_=from_peak[:, :, :width], func=ACT.Square, bias=-2.0
             )
-            neg_hat = work.tile([P, 2, CHUNK], F32)
-            nc.vector.tensor_scalar(
-                out=neg_hat[:, :, :width],
-                in0=from_peak[:, :, :width],
-                scalar1=2.0,
-                scalar2=0.0,
-                op0=ALU.subtract,
-                op1=ALU.min,
-            )
-            outer = work.tile([P, 2, CHUNK], F32)
-            nc.vector.scalar_tensor_tensor(
-                out=outer[:, :, :width],
-                in0=neg_hat[:, :, :width],
-                scalar=-1.0 / 6.0,
-                in1=hat_sq[:, :, :width],
-                op0=ALU.mult,
-                op1=ALU.mult,
-            )
-            inner = work.tile([P, 2, CHUNK], F32)
-            nc.vector.scalar_tensor_tensor(
-                out=inner[:, :, :width],
-                in0=neg_hat[:, :, :width],
-                scalar=0.5,
-                in1=peak_sq[:, :, :width],
-                op0=ALU.mult,
-                op1=ALU.mult,
-            )
-            bump = work.tile([P, 2, CHUNK], BF16)
-            nc.vector.scalar_tensor_tensor(
-                out=bump[:, :, :width],
-                in0=inner[:, :, :width],
-                scalar=2.0 / 3.0,
-                in1=outer[:, :, :width],
-                op0=ALU.add,
-                op1=ALU.min,
-            )
-            signed = work.tile([P, 4, CHUNK], BF16)
-            nc.vector.tensor_tensor(
-                out=signed[:, 2:4, :width],
-                in0=bump[:, :, :width],
-                in1=side[:, :, :width],
-                op=ALU.mult,
-            )
-            nc.vector.tensor_scalar(
-                out=signed[:, 0:2, :width],
-                in0=signed[:, 2:4, :width],
-                scalar1=-1.0,
-                scalar2=None,
-                op0=ALU.mult,
-            )
-            grouped = work.tile([P, CHUNK, 4], BF16, align_bytes=64)
-            nc.vector.tensor_scalar(
-                out=grouped[:, :width].rearrange("p (c i) t -> p c t i", i=RUN),
-                in0=signed[:, :, :width].rearrange("p t (c i) -> p c t i", i=RUN),
-                scalar1=0.0,
-                scalar2=None,
-                op0=ALU.max,
-            )
-            columns = slice(start, start + width)
-            nc.vector.quantize_mx(
-                out=sb_codes[:, columns].bitcast(FP8X4),
-                scales=sb_scales[:, columns],
-                in_=grouped[:, :width].rearrange("p n t -> p (n t)"),
-            )
-            nc.vector.tensor_copy(
-                out=sb_scales_moved[:, start + IMAGES : start + IMAGES + width].bitcast(I32),
-                in_=sb_scales[:, columns].bitcast(I32),
-            )
+            scalar_out_of[i] = (side, peak_sq, hat, hat_sq)
 
-        def output_row(p):
+        def vector_part(i):
+            start, width = starts[i], widths[i]
+            side, peak_sq, hat, hat_sq = scalar_out_of[i]
+            halves = ((0, width // 2), (width // 2, width))
+            outer = work.tile([P, 2, CHUNK], F32)
+            for c0, c1 in halves:
+                nc.vector.scalar_tensor_tensor(
+                    out=outer[:, :, c0:c1],
+                    in0=hat[:, :, c0:c1],
+                    scalar=1.0 / 6.0,
+                    in1=hat_sq[:, :, c0:c1],
+                    op0=ALU.mult,
+                    op1=ALU.mult,
+                )
+            inner = work.tile([P, 2, CHUNK], F32)
+            for c0, c1 in halves:
+                nc.vector.scalar_tensor_tensor(
+                    out=inner[:, :, c0:c1],
+                    in0=hat[:, :, c0:c1],
+                    scalar=-0.5,
+                    in1=peak_sq[:, :, c0:c1],
+                    op0=ALU.mult,
+                    op1=ALU.mult,
+                )
+            bump = work.tile([P, 2, CHUNK], BF16)
+            for c0, c1 in halves:
+                nc.vector.scalar_tensor_tensor(
+                    out=bump[:, :, c0:c1],
+                    in0=inner[:, :, c0:c1],
+                    scalar=2.0 / 3.0,
+                    in1=outer[:, :, c0:c1],
+                    op0=ALU.add,
+                    op1=ALU.min,
+                )
+            signed = work.tile([P, 4, CHUNK], BF16)
+            for c0, c1 in halves:
+                nc.vector.tensor_tensor(
+                    out=signed[:, 2:4, c0:c1], in0=bump[:, :, c0:c1], in1=side[:, :, c0:c1], op=ALU.mult
+                )
+            for c0, c1 in halves:
+                nc.vector.tensor_scalar(
+                    out=signed[:, 0:2, c0:c1],
+                    in0=signed[:, 2:4, c0:c1],
+                    scalar1=-1.0,
+                    scalar2=None,
+                    op0=ALU.mult,
+                )
+            grouped = work.tile([P, CHUNK, 4], BF16, align_bytes=64)
+            for c0, c1 in halves:
+                nc.vector.tensor_scalar(
+                    out=grouped[:, c0:c1].rearrange("p (c i) t -> p c t i", i=RUN),
+                    in0=signed[:, :, c0:c1].rearrange("p t (c i) -> p c t i", i=RUN),
+                    scalar1=0.0,
+                    scalar2=None,
+                    op0=ALU.max,
+                )
+            for c0, c1 in halves:
+                nc.vector.quantize_mx(
+                    out=sb_codes[:, start + c0 : start + c1].bitcast(FP8X4),
+                    scales=sb_scales[:, start + c0 : start + c1],
+                    in_=grouped[:, c0:c1].rearrange("p n t -> p (n t)"),
+                )
+            for c0, c1 in halves:
+                nc.vector.tensor_copy(
+                    out=sb_scales_moved[:, start + IMAGES + c0 : start + IMAGES + c1].bitcast(I32),
+                    in_=sb_scales[:, start + c0 : start + c1].bitcast(I32),
+                )
+
+        acc_of = {}
+        added_of = {}
+
+        def multiply_row(p):
             acc = psum_out.tile([P, Q_TILES, F], F32)
             for t in range(Q_TILES):
                 for tap in range(TAPS):
@@ -247,31 +279,54 @@ def tile_conv2dkan_pa_t_kernel(
                         stop=(tap == TAPS - 1),
                     )
             added = work.tile([P, Q_TILES, F], F32)
-            nc.gpsimd.tensor_tensor(
+            nc.vector.tensor_tensor(
                 out=added[:],
                 in0=base_tiles[:, p * Q_TILES : (p + 1) * Q_TILES, :],
                 in1=bias_rows[:].unsqueeze(1).to_broadcast([P, Q_TILES, F]),
                 op=ALU.add,
             )
-            result = work.tile([P, Q_TILES, F], F32)
-            nc.vector.tensor_tensor(out=result[:], in0=acc[:], in1=added[:], op=ALU.add)
-            for j in range(SPOTS_PER_TILE):
-                nc.sync.dma_start(
-                    out=out_view[j, :, p], in_=result[j * IMAGES : (j + 1) * IMAGES]
-                )
+            acc_of[p] = acc
+            added_of[p] = added
 
-        starts = list(range(0, COLS, CHUNK))
-        widths = [min(CHUNK, COLS - start) for start in starts]
-        next_row = 0
-        z_next = knot_offsets(starts[0], widths[0])
-        for i, start in enumerate(starts):
-            z_now = z_next
-            if i + 1 < len(starts):
-                z_next = knot_offsets(starts[i + 1], widths[i + 1])
-            while (next_row + 3) * ROW_COLS <= start:
-                output_row(next_row)
-                next_row += 1
-            quantised_basis(start, widths[i], z_now)
-        while next_row < OUT_SIDE:
-            output_row(next_row)
-            next_row += 1
+        def finish_row(p):
+            result = work.tile([P, Q_TILES, F], F32)
+            nc.vector.tensor_tensor(out=result[:], in0=acc_of[p][:], in1=added_of[p][:], op=ALU.add)
+            for j in range(SPOTS_PER_TILE):
+                nc.sync.dma_start(out=out_view[j, :, p], in_=result[j * IMAGES : (j + 1) * IMAGES])
+
+        def rows_complete(columns):
+            return min(max(columns // ROW_COLS - 2, 0), OUT_SIDE)
+
+        transpose_x(0)
+        copy_x_t(0)
+        knot_offsets(0)
+        transpose_x(1)
+        copy_x_t(1)
+        multiplied = 0
+        finished = 0
+        for i in range(chunks):
+            if i + 1 < chunks:
+                knot_offsets(i + 1)
+            if i + 2 < chunks:
+                transpose_x(i + 2)
+            scalar_part(i)
+            if i + 2 < chunks:
+                copy_x_t(i + 2)
+            if i == 0:
+                nc.vector.tensor_tensor(
+                    out=bias_rows[:], in0=kan_rows[:], in1=conv_rows[:], op=ALU.add
+                )
+            vector_part(i)
+            ready = multiplied
+            while multiplied < rows_complete(starts[i]):
+                multiply_row(multiplied)
+                multiplied += 1
+            while finished < ready:
+                finish_row(finished)
+                finished += 1
+        while multiplied < OUT_SIDE:
+            multiply_row(multiplied)
+            multiplied += 1
+        while finished < OUT_SIDE:
+            finish_row(finished)
+            finished += 1

@@ -23,7 +23,7 @@ SPOTS_PER_TILE = P // IMAGES
 BLOCKS = COLS // P
 CHUNK = 512
 Q_TILES = OUT_SIDE // SPOTS_PER_TILE
-RUN = 4
+BANK_COLS = CHUNK // 2
 X_LOADS = 4
 
 FLOPS = 2 * IMAGES * OUT_SIDE * OUT_SIDE * TAPS * C * 8 * F
@@ -143,48 +143,46 @@ def tile_conv2dkan_pa_t_kernel(
 
         def knot_offsets(i):
             z_of[i] = []
-            for lo in range(2):
+            for first in range(0, widths[i], BANK_COLS):
+                cols = min(BANK_COLS, widths[i] - first)
                 z = psum_z.tile([P, CHUNK], F32, name="z")
-                nc.tensor.matmul(
-                    z[:, : widths[i]],
-                    lhsT=to_z[:, lo].rearrange("r c hi -> r (c hi)"),
-                    rhs=x_t_of[i][:, : widths[i]],
-                    start=True,
-                    stop=True,
-                )
-                z_of[i].append(z)
+                for lo in range(2):
+                    nc.tensor.matmul(
+                        z[:, lo : 2 * cols : 2],
+                        lhsT=to_z[:, lo].rearrange("r c hi -> r (c hi)"),
+                        rhs=x_t_of[i][:, first : first + cols],
+                        start=True,
+                        stop=True,
+                    )
+                z_of[i].append((z, first, cols))
 
         def scalar_part(i):
-            width = widths[i]
-            from_knot = work.tile([P, 2, CHUNK], F32)
-            side = work.tile([P, 2, CHUNK], BF16)
-            for lo in range(2):
+            count = 2 * widths[i]
+            from_knot = work.tile([P, 2 * CHUNK], F32)
+            side = work.tile([P, 2 * CHUNK], BF16)
+            for z, first, cols in z_of[i]:
                 nc.scalar.activation(
-                    out=from_knot[:, lo, :width], in_=z_of[i][lo][:, :width], func=ACT.Abs
+                    out=from_knot[:, 2 * first : 2 * (first + cols)], in_=z[:, : 2 * cols], func=ACT.Abs
                 )
-            for lo in range(2):
+            for z, first, cols in z_of[i]:
                 nc.scalar.activation(
-                    out=side[:, lo, :width], in_=z_of[i][lo][:, :width], func=ACT.Sign
+                    out=side[:, 2 * first : 2 * (first + cols)], in_=z[:, : 2 * cols], func=ACT.Sign
                 )
-            from_peak = work.tile([P, 2, CHUNK], F32)
+            from_peak = work.tile([P, 2 * CHUNK], F32)
             nc.scalar.activation(
-                out=from_peak[:, :, :width], in_=from_knot[:, :, :width], func=ACT.Abs, bias=-2.0
+                out=from_peak[:, :count], in_=from_knot[:, :count], func=ACT.Abs, bias=-2.0
             )
-            peak_sq = work.tile([P, 2, CHUNK], F32)
+            peak_sq = work.tile([P, 2 * CHUNK], F32)
             nc.scalar.activation(
-                out=peak_sq[:, :, :width], in_=from_knot[:, :, :width], func=ACT.Square, bias=-2.0
+                out=peak_sq[:, :count], in_=from_knot[:, :count], func=ACT.Square, bias=-2.0
             )
-            hat = work.tile([P, 2, CHUNK], F32)
+            hat = work.tile([P, 2 * CHUNK], F32)
             nc.scalar.activation(
-                out=hat[:, :, :width],
-                in_=from_peak[:, :, :width],
-                func=ACT.Relu,
-                bias=2.0,
-                scale=-1.0,
+                out=hat[:, :count], in_=from_peak[:, :count], func=ACT.Relu, bias=2.0, scale=-1.0
             )
-            hat_sq = work.tile([P, 2, CHUNK], F32)
+            hat_sq = work.tile([P, 2 * CHUNK], F32)
             nc.scalar.activation(
-                out=hat_sq[:, :, :width], in_=from_peak[:, :, :width], func=ACT.Square, bias=-2.0
+                out=hat_sq[:, :count], in_=from_peak[:, :count], func=ACT.Square, bias=-2.0
             )
             scalar_out_of[i] = (side, peak_sq, hat, hat_sq)
 
@@ -192,57 +190,41 @@ def tile_conv2dkan_pa_t_kernel(
             start, width = starts[i], widths[i]
             side, peak_sq, hat, hat_sq = scalar_out_of[i]
             halves = ((0, width // 2), (width // 2, width))
-            outer = work.tile([P, 2, CHUNK], F32)
+            outer = work.tile([P, 2 * CHUNK], F32)
             for c0, c1 in halves:
                 nc.vector.scalar_tensor_tensor(
-                    out=outer[:, :, c0:c1],
-                    in0=hat[:, :, c0:c1],
-                    scalar=1.0 / 6.0,
-                    in1=hat_sq[:, :, c0:c1],
-                    op0=ALU.mult,
-                    op1=ALU.mult,
+                    out=outer[:, 2 * c0 : 2 * c1], in0=hat[:, 2 * c0 : 2 * c1], scalar=1.0 / 6.0,
+                    in1=hat_sq[:, 2 * c0 : 2 * c1], op0=ALU.mult, op1=ALU.mult,
                 )
-            inner = work.tile([P, 2, CHUNK], F32)
+            inner = work.tile([P, 2 * CHUNK], F32)
             for c0, c1 in halves:
                 nc.vector.scalar_tensor_tensor(
-                    out=inner[:, :, c0:c1],
-                    in0=hat[:, :, c0:c1],
-                    scalar=-0.5,
-                    in1=peak_sq[:, :, c0:c1],
-                    op0=ALU.mult,
-                    op1=ALU.mult,
+                    out=inner[:, 2 * c0 : 2 * c1], in0=hat[:, 2 * c0 : 2 * c1], scalar=-0.5,
+                    in1=peak_sq[:, 2 * c0 : 2 * c1], op0=ALU.mult, op1=ALU.mult,
                 )
-            bump = work.tile([P, 2, CHUNK], BF16)
+            bump = work.tile([P, 2 * CHUNK], BF16)
             for c0, c1 in halves:
                 nc.vector.scalar_tensor_tensor(
-                    out=bump[:, :, c0:c1],
-                    in0=inner[:, :, c0:c1],
-                    scalar=2.0 / 3.0,
-                    in1=outer[:, :, c0:c1],
-                    op0=ALU.add,
-                    op1=ALU.min,
+                    out=bump[:, 2 * c0 : 2 * c1], in0=inner[:, 2 * c0 : 2 * c1], scalar=2.0 / 3.0,
+                    in1=outer[:, 2 * c0 : 2 * c1], op0=ALU.add, op1=ALU.min,
                 )
-            signed = work.tile([P, 4, CHUNK], BF16)
+            signed = work.tile([P, 2, 2 * CHUNK], BF16)
             for c0, c1 in halves:
                 nc.vector.tensor_tensor(
-                    out=signed[:, 2:4, c0:c1], in0=bump[:, :, c0:c1], in1=side[:, :, c0:c1], op=ALU.mult
+                    out=signed[:, 1, 2 * c0 : 2 * c1], in0=bump[:, 2 * c0 : 2 * c1],
+                    in1=side[:, 2 * c0 : 2 * c1], op=ALU.mult,
                 )
             for c0, c1 in halves:
                 nc.vector.tensor_scalar(
-                    out=signed[:, 0:2, c0:c1],
-                    in0=signed[:, 2:4, c0:c1],
-                    scalar1=-1.0,
-                    scalar2=None,
-                    op0=ALU.mult,
+                    out=signed[:, 0, 2 * c0 : 2 * c1], in0=signed[:, 1, 2 * c0 : 2 * c1],
+                    scalar1=-1.0, scalar2=None, op0=ALU.mult,
                 )
             grouped = work.tile([P, CHUNK, 4], BF16, align_bytes=64)
             for c0, c1 in halves:
                 nc.vector.tensor_scalar(
-                    out=grouped[:, c0:c1].rearrange("p (c i) t -> p c t i", i=RUN),
-                    in0=signed[:, :, c0:c1].rearrange("p t (c i) -> p c t i", i=RUN),
-                    scalar1=0.0,
-                    scalar2=None,
-                    op0=ALU.max,
+                    out=grouped[:, c0:c1].rearrange("p c (h l) -> p c h l", h=2),
+                    in0=signed[:, :, 2 * c0 : 2 * c1].rearrange("p h (c l) -> p c h l", l=2),
+                    scalar1=0.0, scalar2=None, op0=ALU.max,
                 )
             for c0, c1 in halves:
                 nc.vector.quantize_mx(

@@ -24,7 +24,11 @@ BLOCKS = COLS // P
 CHUNK = 512
 Q_TILES = OUT_SIDE // SPOTS_PER_TILE
 BANK_COLS = CHUNK // 2
-X_LOADS = 4
+CHUNK_BLOCKS = [1, 1, 2] + [4] * 18 + [2, 1, 1, 1]
+FIRST_WEIGHT_ROUND = 3
+WEIGHT_TAPS_A_ROUND = 3
+LAST_MOVES_ON_VECTOR = 4
+X_PIECES = [(0, 4), (4, 8), (8, 16), (16, 32), (32, 56), (56, 81)]
 
 FLOPS = 2 * IMAGES * OUT_SIDE * OUT_SIDE * TAPS * C * 8 * F
 
@@ -37,6 +41,7 @@ def tile_conv2dkan_pa_t_kernel(
         stack.enter_context(tc.manual_schedule())
         keep = stack.enter_context(tc.tile_pool(name="keep", bufs=1))
         work = stack.enter_context(tc.tile_pool(name="work", bufs=2))
+        ring = stack.enter_context(tc.tile_pool(name="ring", bufs=3))
         psum_x = stack.enter_context(tc.psum_pool(name="psum_x", bufs=2))
         psum_z = stack.enter_context(tc.psum_pool(name="psum_z", bufs=4))
         psum_out = stack.enter_context(tc.psum_pool(name="psum_out", bufs=2))
@@ -45,11 +50,9 @@ def tile_conv2dkan_pa_t_kernel(
         x_by_spot = x.rearrange("b h w c -> b (h w) c").rearrange(
             "b (n s) c -> s b n c", s=SPOTS_PER_TILE
         )
-        blocks_per_load = -(-BLOCKS // X_LOADS)
 
         def load_x(piece):
-            first = piece * blocks_per_load
-            last = min(first + blocks_per_load, BLOCKS)
+            first, last = X_PIECES[piece]
             for s in range(SPOTS_PER_TILE):
                 nc.sync.dma_start(
                     out=x_blocks[s * IMAGES : (s + 1) * IMAGES, first:last, 0:C],
@@ -69,19 +72,22 @@ def tile_conv2dkan_pa_t_kernel(
         conv_rows = keep.tile([P, F], BF16)
 
         load_x(0)
+        load_x(1)
+        load_x(2)
         for hi in range(2):
             nc.sync.dma_start(out=factor_raw[hi:P:2], in_=factor_view)
             for half in range(2):
                 nc.sync.dma_start(out=kernel_raw[hi:P:2, half], in_=kernel_view[hi, half])
-        for piece in range(1, X_LOADS):
+        for piece in range(3, len(X_PIECES)):
             load_x(piece)
         nc.sync.dma_start(out=kan_rows[:], in_=kan_bias.partition_broadcast(P))
         nc.sync.dma_start(out=conv_rows[:], in_=conv_bias.partition_broadcast(P))
         for j in range(SPOTS_PER_TILE):
             nc.sync.dma_start(out=base_tiles[j * IMAGES : (j + 1) * IMAGES], in_=base_view[j])
 
-        nc.vector.memset(x_blocks[:, :, C:P], 0.0)
-        nc.vector.memset(x_blocks[:, :, C : C + 1], 1.0)
+        head_blocks = X_PIECES[0][1]
+        nc.vector.memset(x_blocks[:, :head_blocks, C:P], 0.0)
+        nc.vector.memset(x_blocks[:, :head_blocks, C : C + 1], 1.0)
         identity = keep.tile([P, P], BF16)
         make_identity(nc, identity[:])
         to_z = keep.tile([P, 2, C, 2], BF16)
@@ -96,32 +102,38 @@ def tile_conv2dkan_pa_t_kernel(
         for lo in range(2):
             for hi in range(2):
                 nc.vector.memset(to_z[C : C + 1, lo, :, hi], 1.5 - 2 * hi - lo)
+        for first, last in X_PIECES[1:]:
+            nc.gpsimd.memset(x_blocks[:, first:last, C:P], 0.0)
+            nc.gpsimd.memset(x_blocks[:, first:last, C : C + 1], 1.0)
 
         sb_codes = keep.tile([P, COLS], U32, align_bytes=64)
         sb_scales = keep.tile([P, COLS], U8, align_bytes=64)
         sb_scales_moved = keep.tile([P, COLS + 64], U8, align_bytes=64)
-        nc.vector.memset(sb_scales[:].bitcast(I32), 0)
+        nc.gpsimd.memset(sb_scales[:].bitcast(F32), 0.0)
 
         w_grouped = keep.tile([P, TAPS, F, 2, 2], BF16, align_bytes=64)
         w_codes = keep.tile([P, TAPS, F], U32, align_bytes=64)
         w_scales = keep.tile([P, TAPS, F], U8, align_bytes=64)
-        for tap in range(TAPS):
+
+        def multiply_weights(tap):
             nc.vector.tensor_tensor(
                 out=w_grouped[:, tap],
                 in0=kernel_raw[:, :, tap].rearrange("p half lo o -> p o half lo"),
                 in1=factor_raw[:, tap].unsqueeze(2).unsqueeze(3).to_broadcast([P, F, 2, 2]),
                 op=ALU.mult,
             )
-        for tap in range(TAPS):
+
+        def quantize_weights(tap):
             nc.vector.quantize_mx(
                 out=w_codes[:, tap].bitcast(FP8X4),
                 scales=w_scales[:, tap],
                 in_=w_grouped[:, tap].rearrange("p o half lo -> p (o half lo)"),
             )
+
         bias_rows = keep.tile([P, F], F32)
 
-        starts = list(range(0, COLS, CHUNK))
-        widths = [min(CHUNK, COLS - start) for start in starts]
+        widths = [blocks * P for blocks in CHUNK_BLOCKS]
+        starts = [sum(widths[:i]) for i in range(len(widths))]
         chunks = len(starts)
         x_t_psum_of = {}
         x_t_of = {}
@@ -159,7 +171,7 @@ def tile_conv2dkan_pa_t_kernel(
         def scalar_part(i):
             count = 2 * widths[i]
             from_knot = work.tile([P, 2 * CHUNK], F32)
-            side = work.tile([P, 2 * CHUNK], BF16)
+            side = ring.tile([P, 2 * CHUNK], BF16)
             for z, first, cols in z_of[i]:
                 nc.scalar.activation(
                     out=from_knot[:, 2 * first : 2 * (first + cols)], in_=z[:, : 2 * cols], func=ACT.Abs
@@ -186,57 +198,93 @@ def tile_conv2dkan_pa_t_kernel(
             )
             scalar_out_of[i] = (side, peak_sq, hat, hat_sq)
 
-        def vector_part(i):
-            start, width = starts[i], widths[i]
+        bump_of = {}
+        signed_of = {}
+        grouped_of = {}
+        outer_of = {}
+        inner_of = {}
+
+        def v_outer(i):
+            count = 2 * widths[i]
             side, peak_sq, hat, hat_sq = scalar_out_of[i]
-            halves = ((0, width // 2), (width // 2, width))
             outer = work.tile([P, 2 * CHUNK], F32)
-            for c0, c1 in halves:
-                nc.vector.scalar_tensor_tensor(
-                    out=outer[:, 2 * c0 : 2 * c1], in0=hat[:, 2 * c0 : 2 * c1], scalar=1.0 / 6.0,
-                    in1=hat_sq[:, 2 * c0 : 2 * c1], op0=ALU.mult, op1=ALU.mult,
-                )
+            nc.vector.scalar_tensor_tensor(
+                out=outer[:, :count], in0=hat[:, :count], scalar=1.0 / 6.0,
+                in1=hat_sq[:, :count], op0=ALU.mult, op1=ALU.mult,
+            )
+            outer_of[i] = outer
+
+        def v_inner(i):
+            count = 2 * widths[i]
+            side, peak_sq, hat, hat_sq = scalar_out_of[i]
             inner = work.tile([P, 2 * CHUNK], F32)
-            for c0, c1 in halves:
-                nc.vector.scalar_tensor_tensor(
-                    out=inner[:, 2 * c0 : 2 * c1], in0=hat[:, 2 * c0 : 2 * c1], scalar=-0.5,
-                    in1=peak_sq[:, 2 * c0 : 2 * c1], op0=ALU.mult, op1=ALU.mult,
-                )
+            nc.vector.scalar_tensor_tensor(
+                out=inner[:, :count], in0=hat[:, :count], scalar=-0.5,
+                in1=peak_sq[:, :count], op0=ALU.mult, op1=ALU.mult,
+            )
+            inner_of[i] = inner
+
+        def v_bump(i):
+            count = 2 * widths[i]
             bump = work.tile([P, 2 * CHUNK], BF16)
-            for c0, c1 in halves:
-                nc.vector.scalar_tensor_tensor(
-                    out=bump[:, 2 * c0 : 2 * c1], in0=inner[:, 2 * c0 : 2 * c1], scalar=2.0 / 3.0,
-                    in1=outer[:, 2 * c0 : 2 * c1], op0=ALU.add, op1=ALU.min,
-                )
+            nc.vector.scalar_tensor_tensor(
+                out=bump[:, :count], in0=inner_of[i][:, :count], scalar=2.0 / 3.0,
+                in1=outer_of[i][:, :count], op0=ALU.add, op1=ALU.min,
+            )
+            bump_of[i] = bump
+
+        def v_signed(i):
+            count = 2 * widths[i]
+            side = scalar_out_of[i][0]
             signed = work.tile([P, 2, 2 * CHUNK], BF16)
-            for c0, c1 in halves:
-                nc.vector.tensor_tensor(
-                    out=signed[:, 1, 2 * c0 : 2 * c1], in0=bump[:, 2 * c0 : 2 * c1],
-                    in1=side[:, 2 * c0 : 2 * c1], op=ALU.mult,
-                )
-            for c0, c1 in halves:
-                nc.vector.tensor_scalar(
-                    out=signed[:, 0, 2 * c0 : 2 * c1], in0=signed[:, 1, 2 * c0 : 2 * c1],
-                    scalar1=-1.0, scalar2=None, op0=ALU.mult,
-                )
+            nc.vector.tensor_tensor(
+                out=signed[:, 1, :count], in0=bump_of[i][:, :count], in1=side[:, :count], op=ALU.mult
+            )
+            signed_of[i] = signed
+
+        def v_negate(i):
+            count = 2 * widths[i]
+            signed = signed_of[i]
+            nc.vector.tensor_scalar(
+                out=signed[:, 0, :count], in0=signed[:, 1, :count],
+                scalar1=-1.0, scalar2=None, op0=ALU.mult,
+            )
+
+        def v_regroup(i):
+            width = widths[i]
             grouped = work.tile([P, CHUNK, 4], BF16, align_bytes=64)
-            for c0, c1 in halves:
-                nc.vector.tensor_scalar(
-                    out=grouped[:, c0:c1].rearrange("p c (h l) -> p c h l", h=2),
-                    in0=signed[:, :, 2 * c0 : 2 * c1].rearrange("p h (c l) -> p c h l", l=2),
-                    scalar1=0.0, scalar2=None, op0=ALU.max,
-                )
-            for c0, c1 in halves:
-                nc.vector.quantize_mx(
-                    out=sb_codes[:, start + c0 : start + c1].bitcast(FP8X4),
-                    scales=sb_scales[:, start + c0 : start + c1],
-                    in_=grouped[:, c0:c1].rearrange("p n t -> p (n t)"),
-                )
-            for c0, c1 in halves:
-                nc.vector.tensor_copy(
-                    out=sb_scales_moved[:, start + IMAGES + c0 : start + IMAGES + c1].bitcast(I32),
-                    in_=sb_scales[:, start + c0 : start + c1].bitcast(I32),
-                )
+            nc.vector.tensor_scalar(
+                out=grouped[:, :width].rearrange("p c (h l) -> p c h l", h=2),
+                in0=signed_of[i][:, :, : 2 * width].rearrange("p h (c l) -> p c h l", l=2),
+                scalar1=0.0, scalar2=None, op0=ALU.max,
+            )
+            grouped_of[i] = grouped
+
+        def v_quantize(i):
+            start, width = starts[i], widths[i]
+            nc.vector.quantize_mx(
+                out=sb_codes[:, start : start + width].bitcast(FP8X4),
+                scales=sb_scales[:, start : start + width],
+                in_=grouped_of[i][:, :width].rearrange("p n t -> p (n t)"),
+            )
+
+        def v_move(i):
+            start, width = starts[i], widths[i]
+            if i < chunks - LAST_MOVES_ON_VECTOR:
+                return
+            nc.vector.tensor_copy(
+                out=sb_scales_moved[:, start + IMAGES : start + IMAGES + width].bitcast(I32),
+                in_=sb_scales[:, start : start + width].bitcast(I32),
+            )
+
+        def dma_move(i):
+            start, width = starts[i], widths[i]
+            if i >= chunks - LAST_MOVES_ON_VECTOR:
+                return
+            nc.sync.dma_start(
+                out=sb_scales_moved[:, start + IMAGES : start + IMAGES + width].bitcast(I32),
+                in_=sb_scales[:, start : start + width].bitcast(I32),
+            )
 
         acc_of = {}
         added_of = {}
@@ -286,29 +334,49 @@ def tile_conv2dkan_pa_t_kernel(
         copy_x_t(1)
         multiplied = 0
         finished = 0
-        for i in range(chunks):
+        for i in range(chunks + 2):
             if i + 1 < chunks:
                 knot_offsets(i + 1)
             if i + 2 < chunks:
                 transpose_x(i + 2)
-            scalar_part(i)
+            if i < chunks:
+                scalar_part(i)
             if i + 2 < chunks:
                 copy_x_t(i + 2)
-            if i == 0:
+            taps_now = [tap for tap in range(TAPS) if tap // WEIGHT_TAPS_A_ROUND == i - FIRST_WEIGHT_ROUND]
+            for tap in taps_now:
+                multiply_weights(tap)
+            if i == 6:
                 nc.vector.tensor_tensor(
                     out=bias_rows[:], in0=kan_rows[:], in1=conv_rows[:], op=ALU.add
                 )
-            vector_part(i)
+            if 0 <= i - 1 < chunks:
+                v_signed(i - 1)
+            if 0 <= i - 2 < chunks:
+                v_move(i - 2)
+            if i < chunks:
+                v_outer(i)
+            if 0 <= i - 1 < chunks:
+                v_negate(i - 1)
+            if i < chunks:
+                v_inner(i)
+            if 0 <= i - 1 < chunks:
+                v_regroup(i - 1)
+            if i < chunks:
+                v_bump(i)
+            if 0 <= i - 1 < chunks:
+                v_quantize(i - 1)
+                dma_move(i - 1)
+            for tap in taps_now:
+                quantize_weights(tap)
             ready = multiplied
-            while multiplied < rows_complete(starts[i]):
+            moved_columns = starts[i - 2] + widths[i - 2] if i >= 2 else 0
+            while multiplied < rows_complete(moved_columns):
                 multiply_row(multiplied)
                 multiplied += 1
             while finished < ready:
                 finish_row(finished)
                 finished += 1
-        while multiplied < OUT_SIDE:
-            multiply_row(multiplied)
-            multiplied += 1
         while finished < OUT_SIDE:
             finish_row(finished)
             finished += 1

@@ -27,6 +27,7 @@ BANK_COLS = CHUNK // 2
 CHUNK_BLOCKS = [1, 1, 2] + [4] * 18 + [2, 1, 1, 1]
 FIRST_WEIGHT_ROUND = 3
 WEIGHT_TAPS_A_ROUND = 3
+HAT_SHARE = (3, 4)
 LAST_MOVES_ON_VECTOR = 4
 X_PIECES = [(0, 4), (4, 8), (8, 16), (16, 32), (32, 56), (56, 81)]
 
@@ -189,27 +190,44 @@ def tile_conv2dkan_pa_t_kernel(
                 out=peak_sq[:, :count], in_=from_knot[:, :count], func=ACT.Square, bias=-2.0
             )
             hat = work.tile([P, 2 * CHUNK], F32)
-            nc.scalar.activation(
-                out=hat[:, :count], in_=from_peak[:, :count], func=ACT.Relu, bias=2.0, scale=-1.0
-            )
+            if not hat_on_vector(i):
+                nc.scalar.activation(
+                    out=hat[:, :count], in_=from_peak[:, :count], func=ACT.Relu, bias=2.0, scale=-1.0
+                )
             hat_sq = work.tile([P, 2 * CHUNK], F32)
             nc.scalar.activation(
                 out=hat_sq[:, :count], in_=from_peak[:, :count], func=ACT.Square, bias=-2.0
             )
             scalar_out_of[i] = (side, peak_sq, hat, hat_sq)
+            from_peak_of[i] = from_peak
 
         bump_of = {}
+        from_peak_of = {}
+
+        def hat_on_vector(i):
+            return (i * HAT_SHARE[0]) % HAT_SHARE[1] < HAT_SHARE[0]
+
+        def hat_sign(i):
+            return -1.0 if hat_on_vector(i) else 1.0
+
         signed_of = {}
         grouped_of = {}
         outer_of = {}
         inner_of = {}
+
+        def v_hat(i):
+            count = 2 * widths[i]
+            nc.vector.tensor_scalar(
+                out=scalar_out_of[i][2][:, :count], in0=from_peak_of[i][:, :count],
+                scalar1=2.0, scalar2=2.0, op0=ALU.min, op1=ALU.subtract,
+            )
 
         def v_outer(i):
             count = 2 * widths[i]
             side, peak_sq, hat, hat_sq = scalar_out_of[i]
             outer = work.tile([P, 2 * CHUNK], F32)
             nc.vector.scalar_tensor_tensor(
-                out=outer[:, :count], in0=hat[:, :count], scalar=1.0 / 6.0,
+                out=outer[:, :count], in0=hat[:, :count], scalar=hat_sign(i) / 6.0,
                 in1=hat_sq[:, :count], op0=ALU.mult, op1=ALU.mult,
             )
             outer_of[i] = outer
@@ -219,7 +237,7 @@ def tile_conv2dkan_pa_t_kernel(
             side, peak_sq, hat, hat_sq = scalar_out_of[i]
             inner = work.tile([P, 2 * CHUNK], F32)
             nc.vector.scalar_tensor_tensor(
-                out=inner[:, :count], in0=hat[:, :count], scalar=-0.5,
+                out=inner[:, :count], in0=hat[:, :count], scalar=-0.5 * hat_sign(i),
                 in1=peak_sq[:, :count], op0=ALU.mult, op1=ALU.mult,
             )
             inner_of[i] = inner
@@ -350,6 +368,8 @@ def tile_conv2dkan_pa_t_kernel(
                 nc.vector.tensor_tensor(
                     out=bias_rows[:], in0=kan_rows[:], in1=conv_rows[:], op=ALU.add
                 )
+            if i < chunks and hat_on_vector(i):
+                v_hat(i)
             if 0 <= i - 1 < chunks:
                 v_signed(i - 1)
             if 0 <= i - 2 < chunks:

@@ -27,7 +27,9 @@ BANK_COLS = CHUNK // 2
 CHUNK_BLOCKS = [1, 1, 2] + [4] * 18 + [2, 1, 1, 1]
 FIRST_WEIGHT_ROUND = 3
 WEIGHT_TAPS_A_ROUND = 3
-HAT_SHARE = (3, 4)
+HAT_SHARE = (5, 6)
+FIRST_MX_ROUND = FIRST_WEIGHT_ROUND + 3
+ROW_OUT = OUT_SIDE * IMAGES
 LAST_MOVES_ON_VECTOR = 4
 X_PIECES = [(0, 4), (4, 8), (8, 16), (16, 32), (32, 56), (56, 81)]
 
@@ -43,9 +45,10 @@ def tile_conv2dkan_pa_t_kernel(
         keep = stack.enter_context(tc.tile_pool(name="keep", bufs=1))
         work = stack.enter_context(tc.tile_pool(name="work", bufs=2))
         ring = stack.enter_context(tc.tile_pool(name="ring", bufs=3))
-        psum_x = stack.enter_context(tc.psum_pool(name="psum_x", bufs=2))
+        psum_x = stack.enter_context(tc.psum_pool(name="psum_x", bufs=1))
         psum_z = stack.enter_context(tc.psum_pool(name="psum_z", bufs=4))
-        psum_out = stack.enter_context(tc.psum_pool(name="psum_out", bufs=2))
+        psum_acc = stack.enter_context(tc.psum_pool(name="psum_acc", bufs=2))
+        psum_turned = stack.enter_context(tc.psum_pool(name="psum_turned", bufs=1))
 
         x_blocks = keep.tile([P, BLOCKS, P], BF16)
         x_by_spot = x.rearrange("b h w c -> b (h w) c").rearrange(
@@ -91,6 +94,8 @@ def tile_conv2dkan_pa_t_kernel(
         nc.vector.memset(x_blocks[:, :head_blocks, C : C + 1], 1.0)
         identity = keep.tile([P, P], BF16)
         make_identity(nc, identity[:])
+        identity_f32 = keep.tile([P, P], F32)
+        make_identity(nc, identity_f32[:])
         to_z = keep.tile([P, 2, C, 2], BF16)
         for lo in range(2):
             nc.vector.tensor_scalar(
@@ -132,6 +137,7 @@ def tile_conv2dkan_pa_t_kernel(
             )
 
         bias_rows = keep.tile([P, F], F32)
+        bias_column = keep.tile([P, 1], F32)
 
         widths = [blocks * P for blocks in CHUNK_BLOCKS]
         starts = [sum(widths[:i]) for i in range(len(widths))]
@@ -305,66 +311,89 @@ def tile_conv2dkan_pa_t_kernel(
             )
 
         acc_of = {}
-        added_of = {}
+        biased_of = {}
+        turned_of = {}
 
-        def multiply_row(p):
-            acc = psum_out.tile([P, Q_TILES, F], F32)
-            for t in range(Q_TILES):
-                for tap in range(TAPS):
-                    di, dj = divmod(tap, 3)
-                    first = ((p + di) * SIDE + t * SPOTS_PER_TILE + dj) * IMAGES
-                    if first % 64 == 0:
-                        window_scales = sb_scales[:, first : first + P]
-                    else:
-                        window_scales = sb_scales_moved[:, first + IMAGES : first + IMAGES + P]
-                    nc.tensor.matmul_mx(
-                        out=acc[:, t, :],
-                        lhsT=sb_codes[:, first : first + P].bitcast(FP8X4),
-                        lhsT_scale=window_scales,
-                        rhs=w_codes[:, tap].bitcast(FP8X4),
-                        rhs_scale=w_scales[:, tap],
-                        start=(tap == 0),
-                        stop=(tap == TAPS - 1),
-                    )
-            added = work.tile([P, Q_TILES, F], F32)
-            nc.vector.tensor_tensor(
-                out=added[:],
-                in0=base_tiles[:, p * Q_TILES : (p + 1) * Q_TILES, :],
-                in1=bias_rows[:].unsqueeze(1).to_broadcast([P, Q_TILES, F]),
-                op=ALU.add,
+        def window_start(p, tap):
+            di, dj = divmod(tap, 3)
+            return ((p + di) * SIDE + dj) * IMAGES
+
+        def mx_pass(p, tap):
+            if tap == 0:
+                acc_of[p] = psum_acc.tile([P, ROW_OUT], F32, name="acc")
+            first = window_start(p, tap)
+            if first % 64 == 0:
+                window_scales = sb_scales[:, first : first + ROW_OUT]
+            else:
+                window_scales = sb_scales_moved[:, first + IMAGES : first + IMAGES + ROW_OUT]
+            nc.tensor.matmul_mx(
+                out=acc_of[p][:],
+                lhsT=w_codes[:, tap].bitcast(FP8X4),
+                lhsT_scale=w_scales[:, tap],
+                rhs=sb_codes[:, first : first + ROW_OUT].bitcast(FP8X4),
+                rhs_scale=window_scales,
+                start=(tap == 0),
+                stop=(tap == TAPS - 1),
             )
-            acc_of[p] = acc
-            added_of[p] = added
+
+        def add_biases(p):
+            biased = work.tile([P, ROW_OUT], F32)
+            nc.scalar.activation(
+                out=biased[:], in_=acc_of[p][:], func=ACT.Identity, bias=bias_column[:, 0:1]
+            )
+            biased_of[p] = biased
+
+        def turn_row(p):
+            turned = psum_turned.tile([P, Q_TILES, F], F32, name="turned")
+            for t in range(Q_TILES):
+                nc.tensor.transpose(turned[:, t, :], biased_of[p][:, t * P : (t + 1) * P], identity_f32[:])
+            turned_of[p] = turned
 
         def finish_row(p):
             result = work.tile([P, Q_TILES, F], F32)
-            nc.vector.tensor_tensor(out=result[:], in0=acc_of[p][:], in1=added_of[p][:], op=ALU.add)
+            nc.vector.tensor_tensor(
+                out=result[:],
+                in0=turned_of[p][:],
+                in1=base_tiles[:, p * Q_TILES : (p + 1) * Q_TILES, :],
+                op=ALU.add,
+            )
             for j in range(SPOTS_PER_TILE):
                 nc.sync.dma_start(out=out_view[j, :, p], in_=result[j * IMAGES : (j + 1) * IMAGES])
-
-        def rows_complete(columns):
-            return min(max(columns // ROW_COLS - 2, 0), OUT_SIDE)
 
         transpose_x(0)
         copy_x_t(0)
         knot_offsets(0)
         transpose_x(1)
         copy_x_t(1)
-        multiplied = 0
-        finished = 0
-        for i in range(chunks + 2):
+        passes = [(p, tap) for p in range(OUT_SIDE) for tap in range(TAPS)]
+        next_pass = 0
+        summed = []
+        biased = []
+        turned = []
+        for i in range(chunks + 5):
             if i + 1 < chunks:
                 knot_offsets(i + 1)
             if i + 2 < chunks:
                 transpose_x(i + 2)
+            for p in biased:
+                turn_row(p)
+            turned = biased
+            biased = []
+            if i == FIRST_MX_ROUND:
+                bias_turned = psum_turned.tile([P, Q_TILES, F], F32, name="turned")
+                nc.tensor.transpose(bias_turned[:, 0, :], bias_rows[:], identity_f32[:])
             if i < chunks:
                 scalar_part(i)
             if i + 2 < chunks:
                 copy_x_t(i + 2)
+            for p in summed:
+                add_biases(p)
+            biased = summed
+            summed = []
             taps_now = [tap for tap in range(TAPS) if tap // WEIGHT_TAPS_A_ROUND == i - FIRST_WEIGHT_ROUND]
             for tap in taps_now:
                 multiply_weights(tap)
-            if i == 6:
+            if i == FIRST_MX_ROUND - 1:
                 nc.vector.tensor_tensor(
                     out=bias_rows[:], in0=kan_rows[:], in1=conv_rows[:], op=ALU.add
                 )
@@ -389,14 +418,18 @@ def tile_conv2dkan_pa_t_kernel(
                 dma_move(i - 1)
             for tap in taps_now:
                 quantize_weights(tap)
-            ready = multiplied
-            moved_columns = starts[i - 2] + widths[i - 2] if i >= 2 else 0
-            while multiplied < rows_complete(moved_columns):
-                multiply_row(multiplied)
-                multiplied += 1
-            while finished < ready:
-                finish_row(finished)
-                finished += 1
-        while finished < OUT_SIDE:
-            finish_row(finished)
-            finished += 1
+            if i == FIRST_MX_ROUND:
+                nc.vector.tensor_copy(out=bias_column[:], in_=bias_turned[:, 0, 0:1])
+            for p in turned:
+                finish_row(p)
+            turned = []
+            done = min(i - 2, chunks - 1)
+            ready_columns = starts[done] + widths[done] if i >= FIRST_MX_ROUND + 1 else 0
+            while next_pass < len(passes):
+                p, tap = passes[next_pass]
+                if window_start(p, tap) + ROW_OUT > ready_columns:
+                    break
+                mx_pass(p, tap)
+                next_pass += 1
+                if tap == TAPS - 1:
+                    summed.append(p)

@@ -30,6 +30,7 @@ WEIGHT_TAPS_A_ROUND = 3
 HAT_SHARE = (5, 6)
 FIRST_MX_ROUND = FIRST_WEIGHT_ROUND + 3
 ROW_OUT = OUT_SIDE * IMAGES
+HANDED = 3
 LAST_MOVES_ON_VECTOR = 4
 X_PIECES = [(0, 4), (4, 8), (8, 16), (16, 32), (32, 56), (56, 81)]
 
@@ -44,7 +45,9 @@ def tile_conv2dkan_pa_t_kernel(
         stack.enter_context(tc.manual_schedule())
         keep = stack.enter_context(tc.tile_pool(name="keep", bufs=1))
         work = stack.enter_context(tc.tile_pool(name="work", bufs=2))
-        ring = stack.enter_context(tc.tile_pool(name="ring", bufs=3))
+        own = stack.enter_context(tc.tile_pool(name="own", bufs=1))
+        handed = stack.enter_context(tc.tile_pool(name="handed", bufs=HANDED))
+        ring = stack.enter_context(tc.tile_pool(name="ring", bufs=HANDED + 1))
         psum_x = stack.enter_context(tc.psum_pool(name="psum_x", bufs=1))
         psum_z = stack.enter_context(tc.psum_pool(name="psum_z", bufs=4))
         psum_acc = stack.enter_context(tc.psum_pool(name="psum_acc", bufs=2))
@@ -177,7 +180,7 @@ def tile_conv2dkan_pa_t_kernel(
 
         def scalar_part(i):
             count = 2 * widths[i]
-            from_knot = work.tile([P, 2 * CHUNK], F32)
+            from_knot = own.tile([P, 2 * CHUNK], F32)
             side = ring.tile([P, 2 * CHUNK], BF16)
             for z, first, cols in z_of[i]:
                 nc.scalar.activation(
@@ -187,20 +190,20 @@ def tile_conv2dkan_pa_t_kernel(
                 nc.scalar.activation(
                     out=side[:, 2 * first : 2 * (first + cols)], in_=z[:, : 2 * cols], func=ACT.Sign
                 )
-            from_peak = work.tile([P, 2 * CHUNK], F32)
+            from_peak = handed.tile([P, 2 * CHUNK], F32)
             nc.scalar.activation(
                 out=from_peak[:, :count], in_=from_knot[:, :count], func=ACT.Abs, bias=-2.0
             )
-            peak_sq = work.tile([P, 2 * CHUNK], F32)
+            peak_sq = handed.tile([P, 2 * CHUNK], F32)
             nc.scalar.activation(
                 out=peak_sq[:, :count], in_=from_knot[:, :count], func=ACT.Square, bias=-2.0
             )
-            hat = work.tile([P, 2 * CHUNK], F32)
+            hat = handed.tile([P, 2 * CHUNK], F32)
             if not hat_on_vector(i):
                 nc.scalar.activation(
                     out=hat[:, :count], in_=from_peak[:, :count], func=ACT.Relu, bias=2.0, scale=-1.0
                 )
-            hat_sq = work.tile([P, 2 * CHUNK], F32)
+            hat_sq = handed.tile([P, 2 * CHUNK], F32)
             nc.scalar.activation(
                 out=hat_sq[:, :count], in_=from_peak[:, :count], func=ACT.Square, bias=-2.0
             )
@@ -231,7 +234,7 @@ def tile_conv2dkan_pa_t_kernel(
         def v_outer(i):
             count = 2 * widths[i]
             side, peak_sq, hat, hat_sq = scalar_out_of[i]
-            outer = work.tile([P, 2 * CHUNK], F32)
+            outer = own.tile([P, 2 * CHUNK], F32)
             nc.vector.scalar_tensor_tensor(
                 out=outer[:, :count], in0=hat[:, :count], scalar=hat_sign(i) / 6.0,
                 in1=hat_sq[:, :count], op0=ALU.mult, op1=ALU.mult,
@@ -241,7 +244,7 @@ def tile_conv2dkan_pa_t_kernel(
         def v_inner(i):
             count = 2 * widths[i]
             side, peak_sq, hat, hat_sq = scalar_out_of[i]
-            inner = work.tile([P, 2 * CHUNK], F32)
+            inner = own.tile([P, 2 * CHUNK], F32)
             nc.vector.scalar_tensor_tensor(
                 out=inner[:, :count], in0=hat[:, :count], scalar=-0.5 * hat_sign(i),
                 in1=peak_sq[:, :count], op0=ALU.mult, op1=ALU.mult,
@@ -260,7 +263,7 @@ def tile_conv2dkan_pa_t_kernel(
         def v_signed(i):
             count = 2 * widths[i]
             side = scalar_out_of[i][0]
-            signed = work.tile([P, 2, 2 * CHUNK], BF16)
+            signed = own.tile([P, 2, 2 * CHUNK], BF16)
             nc.vector.tensor_tensor(
                 out=signed[:, 1, :count], in0=bump_of[i][:, :count], in1=side[:, :count], op=ALU.mult
             )
@@ -276,7 +279,7 @@ def tile_conv2dkan_pa_t_kernel(
 
         def v_regroup(i):
             width = widths[i]
-            grouped = work.tile([P, CHUNK, 4], BF16, align_bytes=64)
+            grouped = own.tile([P, CHUNK, 4], BF16, align_bytes=64)
             nc.vector.tensor_scalar(
                 out=grouped[:, :width].rearrange("p c (h l) -> p c h l", h=2),
                 in0=signed_of[i][:, :, : 2 * width].rearrange("p h (c l) -> p c h l", l=2),
@@ -423,7 +426,7 @@ def tile_conv2dkan_pa_t_kernel(
             for p in turned:
                 finish_row(p)
             turned = []
-            done = min(i - 2, chunks - 1)
+            done = min(i - 3 if i + 1 < chunks else i - 2, chunks - 1)
             ready_columns = starts[done] + widths[done] if i >= FIRST_MX_ROUND + 1 else 0
             while next_pass < len(passes):
                 p, tap = passes[next_pass]

@@ -25,12 +25,12 @@ CHUNK = 512
 Q_TILES = OUT_SIDE // SPOTS_PER_TILE
 BANK_COLS = CHUNK // 2
 CHUNK_BLOCKS = [1, 1, 2] + [4] * 18 + [2, 1, 1, 1]
-FIRST_WEIGHT_ROUND = 3
-WEIGHT_TAPS_A_ROUND = 3
-HAT_SHARE = (5, 6)
-FIRST_MX_ROUND = FIRST_WEIGHT_ROUND + 3
+WEIGHT_ROUNDS = {1: [0, 1], 2: [2, 3, 4, 5, 6], 3: [7, 8]}
+HAT_SHARE = (1, 1)
+FIRST_MX_ROUND = 6
 ROW_OUT = OUT_SIDE * IMAGES
 HANDED = 3
+LAST_ROWS = 3
 LAST_MOVES_ON_VECTOR = 4
 X_PIECES = [(0, 4), (4, 8), (8, 16), (16, 32), (32, 56), (56, 81)]
 
@@ -347,16 +347,21 @@ def tile_conv2dkan_pa_t_kernel(
             biased_of[p] = biased
 
         def turn_row(p):
-            turned = psum_turned.tile([P, Q_TILES, F], F32, name="turned")
+            if p < OUT_SIDE - LAST_ROWS:
+                turned = psum_turned.tile([P, ROW_OUT], F32, name="turned")
+            else:
+                turned = psum_z.tile([P, CHUNK], F32, name="z")
             for t in range(Q_TILES):
-                nc.tensor.transpose(turned[:, t, :], biased_of[p][:, t * P : (t + 1) * P], identity_f32[:])
+                nc.tensor.transpose(
+                    turned[:, t * F : (t + 1) * F], biased_of[p][:, t * P : (t + 1) * P], identity_f32[:]
+                )
             turned_of[p] = turned
 
         def finish_row(p):
-            result = work.tile([P, Q_TILES, F], F32)
+            result = handed.tile([P, Q_TILES, F], F32)
             nc.vector.tensor_tensor(
                 out=result[:],
-                in0=turned_of[p][:],
+                in0=turned_of[p][:].rearrange("p (t o) -> p t o", t=Q_TILES),
                 in1=base_tiles[:, p * Q_TILES : (p + 1) * Q_TILES, :],
                 op=ALU.add,
             )
@@ -373,6 +378,7 @@ def tile_conv2dkan_pa_t_kernel(
         summed = []
         biased = []
         turned = []
+        waiting = []
         for i in range(chunks + 5):
             if i + 1 < chunks:
                 knot_offsets(i + 1)
@@ -383,8 +389,8 @@ def tile_conv2dkan_pa_t_kernel(
             turned = biased
             biased = []
             if i == FIRST_MX_ROUND:
-                bias_turned = psum_turned.tile([P, Q_TILES, F], F32, name="turned")
-                nc.tensor.transpose(bias_turned[:, 0, :], bias_rows[:], identity_f32[:])
+                bias_turned = psum_turned.tile([P, ROW_OUT], F32, name="turned")
+                nc.tensor.transpose(bias_turned[:, 0:F], bias_rows[:], identity_f32[:])
             if i < chunks:
                 scalar_part(i)
             if i + 2 < chunks:
@@ -393,7 +399,7 @@ def tile_conv2dkan_pa_t_kernel(
                 add_biases(p)
             biased = summed
             summed = []
-            taps_now = [tap for tap in range(TAPS) if tap // WEIGHT_TAPS_A_ROUND == i - FIRST_WEIGHT_ROUND]
+            taps_now = WEIGHT_ROUNDS.get(i, [])
             for tap in taps_now:
                 multiply_weights(tap)
             if i == FIRST_MX_ROUND - 1:
@@ -422,11 +428,14 @@ def tile_conv2dkan_pa_t_kernel(
             for tap in taps_now:
                 quantize_weights(tap)
             if i == FIRST_MX_ROUND:
-                nc.vector.tensor_copy(out=bias_column[:], in_=bias_turned[:, 0, 0:1])
-            for p in turned:
-                finish_row(p)
+                nc.vector.tensor_copy(out=bias_column[:], in_=bias_turned[:, 0:1])
+            waiting.extend(turned)
             turned = []
-            done = min(i - 3 if i + 1 < chunks else i - 2, chunks - 1)
+            if not chunks - 1 <= i <= chunks:
+                for p in waiting:
+                    finish_row(p)
+                waiting = []
+            done = min(i - 3 if i + 2 < chunks else i - 2, chunks - 1)
             ready_columns = starts[done] + widths[done] if i >= FIRST_MX_ROUND + 1 else 0
             while next_pass < len(passes):
                 p, tap = passes[next_pass]

@@ -49,9 +49,9 @@ def tile_conv2dkan_pa_t_kernel(
         handed = stack.enter_context(tc.tile_pool(name="handed", bufs=HANDED))
         ring = stack.enter_context(tc.tile_pool(name="ring", bufs=HANDED + 1))
         psum_x = stack.enter_context(tc.psum_pool(name="psum_x", bufs=1))
-        psum_z = stack.enter_context(tc.psum_pool(name="psum_z", bufs=4))
+        psum_z = stack.enter_context(tc.psum_pool(name="psum_z", bufs=3))
         psum_acc = stack.enter_context(tc.psum_pool(name="psum_acc", bufs=2))
-        psum_turned = stack.enter_context(tc.psum_pool(name="psum_turned", bufs=1))
+        psum_turned = stack.enter_context(tc.psum_pool(name="psum_turned", bufs=2))
 
         x_blocks = keep.tile([P, BLOCKS, P], BF16)
         x_by_spot = x.rearrange("b h w c -> b (h w) c").rearrange(
@@ -186,7 +186,6 @@ def tile_conv2dkan_pa_t_kernel(
                 nc.scalar.activation(
                     out=from_knot[:, 2 * first : 2 * (first + cols)], in_=z[:, : 2 * cols], func=ACT.Abs
                 )
-            for z, first, cols in z_of[i]:
                 nc.scalar.activation(
                     out=side[:, 2 * first : 2 * (first + cols)], in_=z[:, : 2 * cols], func=ACT.Sign
                 )
@@ -380,6 +379,8 @@ def tile_conv2dkan_pa_t_kernel(
         turned = []
         waiting = []
         for i in range(chunks + 5):
+            if i < chunks:
+                scalar_part(i)
             if i + 1 < chunks:
                 knot_offsets(i + 1)
             if i + 2 < chunks:
@@ -391,8 +392,6 @@ def tile_conv2dkan_pa_t_kernel(
             if i == FIRST_MX_ROUND:
                 bias_turned = psum_turned.tile([P, ROW_OUT], F32, name="turned")
                 nc.tensor.transpose(bias_turned[:, 0:F], bias_rows[:], identity_f32[:])
-            if i < chunks:
-                scalar_part(i)
             if i + 2 < chunks:
                 copy_x_t(i + 2)
             for p in summed:

@@ -26,7 +26,7 @@ Q_TILES = OUT_SIDE // SPOTS_PER_TILE
 BANK_COLS = CHUNK // 2
 CHUNK_BLOCKS = [1, 1, 2] + [4] * 18 + [2, 1, 1, 1]
 WEIGHT_ROUNDS = {1: [0, 1], 2: [2, 3, 4, 5, 6], 3: [7, 8]}
-HAT_SHARE = (1, 1)
+HAT_SHARE = (4, 5)
 FIRST_MX_ROUND = 6
 ROW_OUT = OUT_SIDE * IMAGES
 HANDED = 3

from contextlib import ExitStack

import concourse.mybir as mybir
from concourse.masks import make_identity

F32 = mybir.dt.float32
BF16 = mybir.dt.bfloat16
I32 = mybir.dt.int32
U32 = mybir.dt.uint32
U8 = mybir.dt.uint8
FP8X4 = mybir.dt.float8_e4m3fn_x4
ALU = mybir.AluOpType
ACT = mybir.ActivationFunctionType

P = 128
IMAGES, SIDE, C, F = 32, 18, 64, 128
OUT_SIDE = SIDE - 2
TAPS = 9
SPOTS = SIDE * SIDE
COLS = SPOTS * IMAGES
ROW_COLS = SIDE * IMAGES
SPOTS_PER_TILE = P // IMAGES
BLOCKS = COLS // P
CHUNK = 512
Q_TILES = OUT_SIDE // SPOTS_PER_TILE
BANK_COLS = CHUNK // 2
CHUNK_BLOCKS = [1, 1, 2] + [4] * 18 + [2, 1, 1, 1]
WEIGHT_ROUNDS = {1: [0, 1], 2: [2, 3, 4, 5, 6], 3: [7, 8]}
HAT_SHARE = (4, 5)
FIRST_MX_ROUND = 6
ROW_OUT = OUT_SIDE * IMAGES
HANDED = 3
LAST_ROWS = 3
LAST_MOVES_ON_VECTOR = 4
X_PIECES = [(0, 4), (4, 8), (8, 16), (16, 32), (32, 56), (56, 81)]

FLOPS = 2 * IMAGES * OUT_SIDE * OUT_SIDE * TAPS * C * 8 * F


def tile_conv2dkan_pa_t_kernel(
    tc, x, spline_kernel, scale_factor, base, kan_bias, conv_bias, out
):
    nc = tc.nc
    with ExitStack() as stack:
        stack.enter_context(tc.manual_schedule())
        keep = stack.enter_context(tc.tile_pool(name="keep", bufs=1))
        work = stack.enter_context(tc.tile_pool(name="work", bufs=2))
        own = stack.enter_context(tc.tile_pool(name="own", bufs=1))
        handed = stack.enter_context(tc.tile_pool(name="handed", bufs=HANDED))
        ring = stack.enter_context(tc.tile_pool(name="ring", bufs=HANDED + 1))
        psum_x = stack.enter_context(tc.psum_pool(name="psum_x", bufs=1))
        psum_z = stack.enter_context(tc.psum_pool(name="psum_z", bufs=3))
        psum_acc = stack.enter_context(tc.psum_pool(name="psum_acc", bufs=2))
        psum_turned = stack.enter_context(tc.psum_pool(name="psum_turned", bufs=2))

        x_blocks = keep.tile([P, BLOCKS, P], BF16)
        x_by_spot = x.rearrange("b h w c -> b (h w) c").rearrange(
            "b (n s) c -> s b n c", s=SPOTS_PER_TILE
        )

        def load_x(piece):
            first, last = X_PIECES[piece]
            for s in range(SPOTS_PER_TILE):
                nc.sync.dma_start(
                    out=x_blocks[s * IMAGES : (s + 1) * IMAGES, first:last, 0:C],
                    in_=x_by_spot[s, :, first:last, :],
                )

        kernel_raw = keep.tile([P, 2, TAPS, 2, F], BF16)
        factor_raw = keep.tile([P, TAPS, F], BF16)
        kernel_view = spline_kernel.rearrange(
            "(tap c) (half hi lo) o -> hi half c tap lo o", c=C, half=2, hi=2
        )
        factor_view = scale_factor.rearrange("(tap c) o -> c tap o", c=C)
        base_tiles = keep.tile([P, OUT_SIDE * Q_TILES, F], BF16)
        base_view = base.rearrange("b p (t j) o -> j b (p t) o", j=SPOTS_PER_TILE)
        out_view = out.rearrange("b p (t j) o -> j b p t o", j=SPOTS_PER_TILE)
        kan_rows = keep.tile([P, F], BF16)
        conv_rows = keep.tile([P, F], BF16)

        load_x(0)
        load_x(1)
        load_x(2)
        for hi in range(2):
            nc.sync.dma_start(out=factor_raw[hi:P:2], in_=factor_view)
            for half in range(2):
                nc.sync.dma_start(out=kernel_raw[hi:P:2, half], in_=kernel_view[hi, half])
        for piece in range(3, len(X_PIECES)):
            load_x(piece)
        nc.sync.dma_start(out=kan_rows[:], in_=kan_bias.partition_broadcast(P))
        nc.sync.dma_start(out=conv_rows[:], in_=conv_bias.partition_broadcast(P))
        for j in range(SPOTS_PER_TILE):
            nc.sync.dma_start(out=base_tiles[j * IMAGES : (j + 1) * IMAGES], in_=base_view[j])

        head_blocks = X_PIECES[0][1]
        nc.vector.memset(x_blocks[:, :head_blocks, C:P], 0.0)
        nc.vector.memset(x_blocks[:, :head_blocks, C : C + 1], 1.0)
        identity = keep.tile([P, P], BF16)
        make_identity(nc, identity[:])
        identity_f32 = keep.tile([P, P], F32)
        make_identity(nc, identity_f32[:])
        to_z = keep.tile([P, 2, C, 2], BF16)
        for lo in range(2):
            nc.vector.tensor_scalar(
                out=to_z[:, lo],
                in0=identity[:, 0:C].unsqueeze(2).to_broadcast([P, C, 2]),
                scalar1=2.5,
                scalar2=None,
                op0=ALU.mult,
            )
        for lo in range(2):
            for hi in range(2):
                nc.vector.memset(to_z[C : C + 1, lo, :, hi], 1.5 - 2 * hi - lo)
        for first, last in X_PIECES[1:]:
            nc.gpsimd.memset(x_blocks[:, first:last, C:P], 0.0)
            nc.gpsimd.memset(x_blocks[:, first:last, C : C + 1], 1.0)

        sb_codes = keep.tile([P, COLS], U32, align_bytes=64)
        sb_scales = keep.tile([P, COLS], U8, align_bytes=64)
        sb_scales_moved = keep.tile([P, COLS + 64], U8, align_bytes=64)
        nc.gpsimd.memset(sb_scales[:].bitcast(F32), 0.0)

        w_grouped = keep.tile([P, TAPS, F, 2, 2], BF16, align_bytes=64)
        w_codes = keep.tile([P, TAPS, F], U32, align_bytes=64)
        w_scales = keep.tile([P, TAPS, F], U8, align_bytes=64)

        def multiply_weights(tap):
            nc.vector.tensor_tensor(
                out=w_grouped[:, tap],
                in0=kernel_raw[:, :, tap].rearrange("p half lo o -> p o half lo"),
                in1=factor_raw[:, tap].unsqueeze(2).unsqueeze(3).to_broadcast([P, F, 2, 2]),
                op=ALU.mult,
            )

        def quantize_weights(tap):
            nc.vector.quantize_mx(
                out=w_codes[:, tap].bitcast(FP8X4),
                scales=w_scales[:, tap],
                in_=w_grouped[:, tap].rearrange("p o half lo -> p (o half lo)"),
            )

        bias_rows = keep.tile([P, F], F32)
        bias_column = keep.tile([P, 1], F32)

        widths = [blocks * P for blocks in CHUNK_BLOCKS]
        starts = [sum(widths[:i]) for i in range(len(widths))]
        chunks = len(starts)
        x_t_psum_of = {}
        x_t_of = {}
        z_of = {}
        scalar_out_of = {}

        def transpose_x(i):
            x_t_psum = psum_x.tile([P, CHUNK], BF16)
            for n in range(widths[i] // P):
                nc.tensor.transpose(
                    x_t_psum[:, n * P : (n + 1) * P], x_blocks[:, starts[i] // P + n, :], identity[:]
                )
            x_t_psum_of[i] = x_t_psum

        def copy_x_t(i):
            x_t = work.tile([P, CHUNK], BF16)
            nc.scalar.copy(out=x_t[:, : widths[i]], in_=x_t_psum_of[i][:, : widths[i]])
            x_t_of[i] = x_t

        def knot_offsets(i):
            z_of[i] = []
            for first in range(0, widths[i], BANK_COLS):
                cols = min(BANK_COLS, widths[i] - first)
                z = psum_z.tile([P, CHUNK], F32, name="z")
                for lo in range(2):
                    nc.tensor.matmul(
                        z[:, lo : 2 * cols : 2],
                        lhsT=to_z[:, lo].rearrange("r c hi -> r (c hi)"),
                        rhs=x_t_of[i][:, first : first + cols],
                        start=True,
                        stop=True,
                    )
                z_of[i].append((z, first, cols))

        def scalar_part(i):
            count = 2 * widths[i]
            from_knot = own.tile([P, 2 * CHUNK], F32)
            side = ring.tile([P, 2 * CHUNK], BF16)
            for z, first, cols in z_of[i]:
                nc.scalar.activation(
                    out=from_knot[:, 2 * first : 2 * (first + cols)], in_=z[:, : 2 * cols], func=ACT.Abs
                )
                nc.scalar.activation(
                    out=side[:, 2 * first : 2 * (first + cols)], in_=z[:, : 2 * cols], func=ACT.Sign
                )
            from_peak = handed.tile([P, 2 * CHUNK], F32)
            nc.scalar.activation(
                out=from_peak[:, :count], in_=from_knot[:, :count], func=ACT.Abs, bias=-2.0
            )
            peak_sq = handed.tile([P, 2 * CHUNK], F32)
            nc.scalar.activation(
                out=peak_sq[:, :count], in_=from_knot[:, :count], func=ACT.Square, bias=-2.0
            )
            hat = handed.tile([P, 2 * CHUNK], F32)
            if not hat_on_vector(i):
                nc.scalar.activation(
                    out=hat[:, :count], in_=from_peak[:, :count], func=ACT.Relu, bias=2.0, scale=-1.0
                )
            hat_sq = handed.tile([P, 2 * CHUNK], F32)
            nc.scalar.activation(
                out=hat_sq[:, :count], in_=from_peak[:, :count], func=ACT.Square, bias=-2.0
            )
            scalar_out_of[i] = (side, peak_sq, hat, hat_sq)
            from_peak_of[i] = from_peak

        bump_of = {}
        from_peak_of = {}

        def hat_on_vector(i):
            return (i * HAT_SHARE[0]) % HAT_SHARE[1] < HAT_SHARE[0]

        def hat_sign(i):
            return -1.0 if hat_on_vector(i) else 1.0

        signed_of = {}
        grouped_of = {}
        outer_of = {}
        inner_of = {}

        def v_hat(i):
            count = 2 * widths[i]
            nc.vector.tensor_scalar(
                out=scalar_out_of[i][2][:, :count], in0=from_peak_of[i][:, :count],
                scalar1=2.0, scalar2=2.0, op0=ALU.min, op1=ALU.subtract,
            )

        def v_outer(i):
            count = 2 * widths[i]
            side, peak_sq, hat, hat_sq = scalar_out_of[i]
            outer = own.tile([P, 2 * CHUNK], F32)
            nc.vector.scalar_tensor_tensor(
                out=outer[:, :count], in0=hat[:, :count], scalar=hat_sign(i) / 6.0,
                in1=hat_sq[:, :count], op0=ALU.mult, op1=ALU.mult,
            )
            outer_of[i] = outer

        def v_inner(i):
            count = 2 * widths[i]
            side, peak_sq, hat, hat_sq = scalar_out_of[i]
            inner = own.tile([P, 2 * CHUNK], F32)
            nc.vector.scalar_tensor_tensor(
                out=inner[:, :count], in0=hat[:, :count], scalar=-0.5 * hat_sign(i),
                in1=peak_sq[:, :count], op0=ALU.mult, op1=ALU.mult,
            )
            inner_of[i] = inner

        def v_bump(i):
            count = 2 * widths[i]
            bump = work.tile([P, 2 * CHUNK], BF16)
            nc.vector.scalar_tensor_tensor(
                out=bump[:, :count], in0=inner_of[i][:, :count], scalar=2.0 / 3.0,
                in1=outer_of[i][:, :count], op0=ALU.add, op1=ALU.min,
            )
            bump_of[i] = bump

        def v_signed(i):
            count = 2 * widths[i]
            side = scalar_out_of[i][0]
            signed = own.tile([P, 2, 2 * CHUNK], BF16)
            nc.vector.tensor_tensor(
                out=signed[:, 1, :count], in0=bump_of[i][:, :count], in1=side[:, :count], op=ALU.mult
            )
            signed_of[i] = signed

        def v_negate(i):
            count = 2 * widths[i]
            signed = signed_of[i]
            nc.vector.tensor_scalar(
                out=signed[:, 0, :count], in0=signed[:, 1, :count],
                scalar1=-1.0, scalar2=None, op0=ALU.mult,
            )

        def v_regroup(i):
            width = widths[i]
            grouped = own.tile([P, CHUNK, 4], BF16, align_bytes=64)
            nc.vector.tensor_scalar(
                out=grouped[:, :width].rearrange("p c (h l) -> p c h l", h=2),
                in0=signed_of[i][:, :, : 2 * width].rearrange("p h (c l) -> p c h l", l=2),
                scalar1=0.0, scalar2=None, op0=ALU.max,
            )
            grouped_of[i] = grouped

        def v_quantize(i):
            start, width = starts[i], widths[i]
            nc.vector.quantize_mx(
                out=sb_codes[:, start : start + width].bitcast(FP8X4),
                scales=sb_scales[:, start : start + width],
                in_=grouped_of[i][:, :width].rearrange("p n t -> p (n t)"),
            )

        def v_move(i):
            start, width = starts[i], widths[i]
            if i < chunks - LAST_MOVES_ON_VECTOR:
                return
            nc.vector.tensor_copy(
                out=sb_scales_moved[:, start + IMAGES : start + IMAGES + width].bitcast(I32),
                in_=sb_scales[:, start : start + width].bitcast(I32),
            )

        def dma_move(i):
            start, width = starts[i], widths[i]
            if i >= chunks - LAST_MOVES_ON_VECTOR:
                return
            nc.sync.dma_start(
                out=sb_scales_moved[:, start + IMAGES : start + IMAGES + width].bitcast(I32),
                in_=sb_scales[:, start : start + width].bitcast(I32),
            )

        acc_of = {}
        biased_of = {}
        turned_of = {}

        def window_start(p, tap):
            di, dj = divmod(tap, 3)
            return ((p + di) * SIDE + dj) * IMAGES

        def mx_pass(p, tap):
            if tap == 0:
                acc_of[p] = psum_acc.tile([P, ROW_OUT], F32, name="acc")
            first = window_start(p, tap)
            if first % 64 == 0:
                window_scales = sb_scales[:, first : first + ROW_OUT]
            else:
                window_scales = sb_scales_moved[:, first + IMAGES : first + IMAGES + ROW_OUT]
            nc.tensor.matmul_mx(
                out=acc_of[p][:],
                lhsT=w_codes[:, tap].bitcast(FP8X4),
                lhsT_scale=w_scales[:, tap],
                rhs=sb_codes[:, first : first + ROW_OUT].bitcast(FP8X4),
                rhs_scale=window_scales,
                start=(tap == 0),
                stop=(tap == TAPS - 1),
            )

        def add_biases(p):
            biased = work.tile([P, ROW_OUT], F32)
            nc.scalar.activation(
                out=biased[:], in_=acc_of[p][:], func=ACT.Identity, bias=bias_column[:, 0:1]
            )
            biased_of[p] = biased

        def turn_row(p):
            if p < OUT_SIDE - LAST_ROWS:
                turned = psum_turned.tile([P, ROW_OUT], F32, name="turned")
            else:
                turned = psum_z.tile([P, CHUNK], F32, name="z")
            for t in range(Q_TILES):
                nc.tensor.transpose(
                    turned[:, t * F : (t + 1) * F], biased_of[p][:, t * P : (t + 1) * P], identity_f32[:]
                )
            turned_of[p] = turned

        def finish_row(p):
            result = handed.tile([P, Q_TILES, F], F32)
            nc.vector.tensor_tensor(
                out=result[:],
                in0=turned_of[p][:].rearrange("p (t o) -> p t o", t=Q_TILES),
                in1=base_tiles[:, p * Q_TILES : (p + 1) * Q_TILES, :],
                op=ALU.add,
            )
            for j in range(SPOTS_PER_TILE):
                nc.sync.dma_start(out=out_view[j, :, p], in_=result[j * IMAGES : (j + 1) * IMAGES])

        transpose_x(0)
        copy_x_t(0)
        knot_offsets(0)
        transpose_x(1)
        copy_x_t(1)
        passes = [(p, tap) for p in range(OUT_SIDE) for tap in range(TAPS)]
        next_pass = 0
        summed = []
        biased = []
        turned = []
        waiting = []
        for i in range(chunks + 5):
            if i < chunks:
                scalar_part(i)
            if i + 1 < chunks:
                knot_offsets(i + 1)
            if i + 2 < chunks:
                transpose_x(i + 2)
            for p in biased:
                turn_row(p)
            turned = biased
            biased = []
            if i == FIRST_MX_ROUND:
                bias_turned = psum_turned.tile([P, ROW_OUT], F32, name="turned")
                nc.tensor.transpose(bias_turned[:, 0:F], bias_rows[:], identity_f32[:])
            if i + 2 < chunks:
                copy_x_t(i + 2)
            for p in summed:
                add_biases(p)
            biased = summed
            summed = []
            taps_now = WEIGHT_ROUNDS.get(i, [])
            for tap in taps_now:
                multiply_weights(tap)
            if i == FIRST_MX_ROUND - 1:
                nc.vector.tensor_tensor(
                    out=bias_rows[:], in0=kan_rows[:], in1=conv_rows[:], op=ALU.add
                )
            if i < chunks and hat_on_vector(i):
                v_hat(i)
            if 0 <= i - 1 < chunks:
                v_signed(i - 1)
            if 0 <= i - 2 < chunks:
                v_move(i - 2)
            if i < chunks:
                v_outer(i)
            if 0 <= i - 1 < chunks:
                v_negate(i - 1)
            if i < chunks:
                v_inner(i)
            if 0 <= i - 1 < chunks:
                v_regroup(i - 1)
            if i < chunks:
                v_bump(i)
            if 0 <= i - 1 < chunks:
                v_quantize(i - 1)
                dma_move(i - 1)
            for tap in taps_now:
                quantize_weights(tap)
            if i == FIRST_MX_ROUND:
                nc.vector.tensor_copy(out=bias_column[:], in_=bias_turned[:, 0:1])
            waiting.extend(turned)
            turned = []
            if not chunks - 1 <= i <= chunks:
                for p in waiting:
                    finish_row(p)
                waiting = []
            done = min(i - 3 if i + 2 < chunks else i - 2, chunks - 1)
            ready_columns = starts[done] + widths[done] if i >= FIRST_MX_ROUND + 1 else 0
            while next_pass < len(passes):
                p, tap = passes[next_pass]
                if window_start(p, tap) + ROW_OUT > ready_columns:
                    break
                mx_pass(p, tap)
                next_pass += 1
                if tap == TAPS - 1:
                    summed.append(p)
